import numpy as np
import ml_dtypes


def mxq(x, axis, fmt="e4m3"):
    dtype, down = {"e4m3": (ml_dtypes.float8_e4m3fn, 7), "e5m2": (ml_dtypes.float8_e5m2, 14)}[fmt]
    v = np.moveaxis(np.asarray(x, np.float32).astype(ml_dtypes.bfloat16).astype(np.float64), axis, -1)
    blocks = v.reshape(v.shape[:-1] + (-1, 32))
    amax = np.abs(blocks).max(-1, keepdims=True)
    byte = np.maximum(np.where(amax > 0, np.frexp(amax)[1] - 1 + 127, 0) - down, 1)
    scale = np.exp2(byte - 127.0)
    codes = (blocks / scale).astype(np.float32).astype(dtype).astype(np.float64)
    return np.moveaxis((codes * scale).reshape(v.shape), -1, axis)


WIDE = False


def mx_kscale(k):
    if not WIDE:
        return np.ones(k)
    levels = np.array([10, -10, 5, -5, 0])
    a = np.random.permutation(np.resize(levels, k // 512 * 4)).reshape(k // 512, 4)
    idx = np.arange(k)
    return np.exp2(a[idx // 512, idx % 128 // 32])


BF16 = ml_dtypes.bfloat16


def bf(x):
    return np.asarray(x, np.float32).astype(BF16)


def f64(x):
    return np.asarray(x).astype(np.float64)


B, L, D, H, KV, HD, QB = 1, 1024, 1024, 4, 2, 256, 512
REP = H // KV
NB = L // QB


def unit(g):
    return g / np.sqrt(np.sum(np.square(g), axis=-1, keepdims=True))


def setup_inputs():
    t = mx_kscale(H * HD).reshape(H, HD)[::REP]
    tw = np.repeat(t, REP, axis=0).reshape(H * HD)
    m = 0.5 * np.random.standard_normal((1, KV, 1, HD))
    return {"q_n": bf(unit(np.random.standard_normal((B, H, L, HD)))),
            "k_n": bf(unit(np.random.standard_normal((B, KV, L, HD)))),
            "v": bf((np.random.standard_normal((B, KV, L, HD)) + m) * t[None, :, None, :]),
            "Wo": bf(np.random.standard_normal((H * HD, D)) * 2.0 / np.sqrt(H * HD) / tw[:, None]),
            "x": bf(np.random.standard_normal((B, L, D)) * np.exp(0.5 * np.random.standard_normal((B, L, 1)))),
            "gate": bf(0.7 + 0.03 * np.random.standard_normal(1)),
            "log_temperature": bf(0.5 * np.log(HD) + 0.03 * np.random.standard_normal(1))}


def reference(q_n, k_n, v, Wo, x, gate, log_temperature):
    q = f64(q_n).reshape(B, KV, REP, L, HD)
    k = f64(k_n)[:, :, None]
    vq = mxq(f64(v), 2, "e4m3")[:, :, None]
    scale = np.exp(f64(log_temperature))
    rows = []
    for i in range(NB):
        lo, hi = i * QB, (i + 1) * QB
        s = (q[:, :, :, lo:hi] @ k[:, :, :, :hi].transpose(0, 1, 2, 4, 3)) * scale
        keep = np.arange(lo, hi)[:, None] >= np.arange(hi)[None, :]
        s = np.where(keep, s, -np.inf)
        e = np.exp(s - s.max(-1, keepdims=True))
        rows.append((mxq(e, 4, "e4m3") @ vq[:, :, :, :hi]) / e.sum(-1, keepdims=True))
    a = np.concatenate(rows, axis=3).reshape(B, H, L, HD).transpose(0, 2, 1, 3).reshape(B, L, H * HD)
    out = mxq(a, 2, "e4m3") @ mxq(f64(Wo), 0, "e4m3")
    return f64(x) + f64(gate) * out

@@ -1,0 +1,408 @@
+from contextlib import ExitStack
+
+import concourse.mybir as mybir
+from concourse.masks import make_identity
+
+F32 = mybir.dt.float32
+BF16 = mybir.dt.bfloat16
+U32 = mybir.dt.uint32
+U8 = mybir.dt.uint8
+FP8X4 = mybir.dt.float8_e4m3fn_x4
+ALU = mybir.AluOpType
+FUNC = mybir.ActivationFunctionType
+AXIS_X = mybir.AxisListType.X
+
+P = 128
+L = 1024
+HD = 256
+H = 4
+KV = 2
+D = 1024
+PAIR = H // KV
+Q_TILES = L // P
+K_PASS = 512
+BANK = 512
+HALF = 256
+MASKED = -1.0e30
+WO_FIRST_SLOT = 4
+V_SECOND_SLOT = 6
+PROJECT_LAG = 3
+
+FLOPS = 2 * H * (512 * 512 + 512 * 1024) * HD * 2 + 2 * L * D * D
+
+
+def tile_sharedglobalattention_pb_kernel(tc, q_n, k_n, v, Wo, x, gate, log_temperature, out):
+    nc = tc.nc
+    with ExitStack() as ctx:
+        const = ctx.enter_context(tc.tile_pool(name="const", bufs=1))
+        resident = ctx.enter_context(tc.tile_pool(name="resident", bufs=1))
+        work = ctx.enter_context(tc.tile_pool(name="work", bufs=3))
+        small = ctx.enter_context(tc.tile_pool(name="small", bufs=4))
+        psum_s = ctx.enter_context(tc.psum_pool(name="psum_s", bufs=4))
+        psum_t = ctx.enter_context(tc.psum_pool(name="psum_t", bufs=2))
+        psum_acc = ctx.enter_context(tc.psum_pool(name="psum_acc", bufs=2))
+        ctx.enter_context(tc.manual_schedule())
+
+        q_raw = resident.tile([P, Q_TILES, H, HD], BF16, name="q_raw")
+        k_raw = resident.tile([P, KV, Q_TILES, HD], BF16, name="k_raw")
+        v_raw = resident.tile([P, KV * L * HD // P], BF16, name="v_raw")
+        wo_raw = resident.tile([P, D * D // P], BF16, name="wo_raw")
+        x_sb = resident.tile([P, Q_TILES, D], BF16, name="x_sb")
+        q_t = resident.tile([P, Q_TILES, H, P], F32, name="q_t")
+        k_t = resident.tile([P, KV, L], F32, name="k_t")
+        v_codes = resident.tile([P, KV * 2 * HD], U32, name="v_codes", align_bytes=64)
+        v_scales = resident.tile([P, KV * 2 * HD], U8, name="v_scales", align_bytes=64)
+        wo_codes = resident.tile([P, 2 * D], U32, name="wo_codes", align_bytes=64)
+        wo_scales = resident.tile([P, 2 * D], U8, name="wo_scales", align_bytes=64)
+        e_tiles = []
+        a_tiles = []
+        for i in range(Q_TILES):
+            e_tiles.append(resident.tile([P, H, K_PASS * (i // 4 + 1)], BF16, name="e%d" % i))
+            a_tiles.append(resident.tile([P, D], BF16, name="a%d" % i))
+
+        lt_bf = const.tile([P, 1], BF16, name="lt_bf")
+        gate_bf = const.tile([P, 1], BF16, name="gate_bf")
+        nc.sync.dma_start(out=lt_bf[:], in_=log_temperature.partition_broadcast(P))
+        nc.sync.dma_start(out=gate_bf[:], in_=gate.partition_broadcast(P))
+
+        def load_k(i):
+            for g in range(KV):
+                nc.sync.dma_start(
+                    out=k_raw[:, g, i : i + 2, :],
+                    in_=k_n[0, g, i * P : (i + 2) * P, :].rearrange("(t p) d -> p t d", p=P),
+                )
+
+        def load_q(i):
+            nc.sync.dma_start(
+                out=q_raw[:, i, :, :], in_=q_n[0, :, i * P : (i + 1) * P, :].rearrange("n p d -> p n d")
+            )
+
+        def load_v(c):
+            for g in range(KV):
+                cols = slice((g * 2 + c) * 4 * HD, (g * 2 + c + 1) * 4 * HD)
+                nc.sync.dma_start(
+                    out=v_raw[:, cols].rearrange("p (u e d) -> p u e d", e=2, d=HD),
+                    in_=v[0, g, c * K_PASS : (c + 1) * K_PASS, :].rearrange("(u p e) d -> p u e d", p=P, e=2),
+                )
+
+        def load_wo():
+            for g in range(2):
+                nc.sync.dma_start(
+                    out=wo_raw[:, g * 4 * D : (g + 1) * 4 * D].rearrange("p (u e n) -> p u e n", e=2, n=D),
+                    in_=Wo[g * K_PASS : (g + 1) * K_PASS, :].rearrange("(u p e) n -> p u e n", p=P, e=2),
+                )
+
+        def load_x(i):
+            nc.sync.dma_start(out=x_sb[:, i, :], in_=x[0, i * P : (i + 1) * P, :])
+
+        load_k(0)
+        load_q(0)
+        load_v(0)
+        load_q(1)
+        load_k(2)
+        load_q(2)
+        load_q(3)
+        load_wo()
+        load_k(4)
+        load_v(1)
+        for i in range(4, Q_TILES):
+            if i == 6:
+                load_k(i)
+            load_q(i)
+            load_x(i - 4)
+        for i in range(4, Q_TILES):
+            load_x(i)
+
+        ident_f32 = const.tile([P, P], F32, name="ident_f32")
+        make_identity(nc, ident_f32[:])
+        ident_bf = const.tile([P, P], BF16, name="ident_bf")
+        make_identity(nc, ident_bf[:])
+        mask_f32 = const.tile([P, P], F32, name="mask_f32")
+        nc.gpsimd.memset(mask_f32[:], 0.0)
+        nc.gpsimd.affine_select(
+            out=mask_f32[:],
+            in_=mask_f32[:],
+            compare_op=ALU.is_ge,
+            fill=MASKED,
+            base=0,
+            pattern=[[-1, P]],
+            channel_multiplier=1,
+        )
+        mask_bf = const.tile([P, P], BF16, name="mask_bf")
+        nc.vector.tensor_copy(out=mask_bf[:], in_=mask_f32[:])
+        for i in range(Q_TILES):
+            keys = (i + 1) * P
+            if keys < K_PASS * (i // 4 + 1):
+                nc.gpsimd.memset(e_tiles[i][:, :, keys:], 0.0)
+
+        scale = const.tile([P, 1], F32, name="scale")
+        nc.scalar.activation(out=scale[:], in_=lt_bf[:], func=FUNC.Exp)
+        neg_scale = const.tile([P, 1], F32, name="neg_scale")
+        nc.vector.tensor_scalar(out=neg_scale[:], in0=scale[:], scalar1=-1.0, scalar2=None, op0=ALU.mult)
+        gate_f = const.tile([P, 1], F32, name="gate_f")
+        nc.vector.tensor_copy(out=gate_f[:], in_=gate_bf[:])
+
+        def regroup(raw, width):
+            grouped = work.tile([P, 4 * BANK], BF16, name="grouped", align_bytes=64)
+            nc.vector.tensor_copy(
+                out=grouped[:, : 4 * width].rearrange("p (c i t) -> p c t i", i=4, t=4),
+                in_=raw.rearrange("p t (c i) -> p c t i", i=4),
+            )
+            return grouped
+
+        def prepare_v(c):
+            grouped = []
+            for g in range(KV):
+                cols = slice((g * 2 + c) * 4 * HD, (g * 2 + c + 1) * 4 * HD)
+                grouped.append(regroup(v_raw[:, cols].rearrange("p (t d) -> p t d", t=4), HD))
+            for g in range(KV):
+                cols = slice((g * 2 + c) * HD, (g * 2 + c + 1) * HD)
+                nc.vector.quantize_mx(
+                    out=v_codes[:, cols].bitcast(FP8X4), scales=v_scales[:, cols], in_=grouped[g][:, : 4 * HD]
+                )
+
+        wo_grouped = {}
+
+        def regroup_wo(w):
+            g, half = w // 2, w % 2
+            raw = wo_raw[:, g * 4 * D : (g + 1) * 4 * D].rearrange("p (t n) -> p t n", t=4)
+            wo_grouped[w] = regroup(raw[:, :, half * BANK : (half + 1) * BANK], BANK)
+
+        def quantise_wo(w):
+            cols = slice(w * BANK, (w + 1) * BANK)
+            nc.vector.quantize_mx(out=wo_codes[:, cols].bitcast(FP8X4), scales=wo_scales[:, cols], in_=wo_grouped[w][:])
+
+        def halves(words):
+            return words.bitcast(BF16).rearrange("p (c e) -> p c e", e=2)
+
+        def transpose_q(i):
+            bank = psum_t.tile([P, H, P], F32, name="bank_q", tag="t")
+            for n in range(H):
+                nc.tensor.transpose(bank[:, n, :], q_raw[:, i, n, :].bitcast(F32), ident_f32[:])
+            nc.scalar.copy(out=q_t[:, i, :, :], in_=bank[:])
+
+        def transpose_k(i):
+            bank = psum_t.tile([P, KV, 2, P], F32, name="bank_k", tag="t")
+            for g in range(KV):
+                for t in range(2):
+                    nc.tensor.transpose(bank[:, g, t, :], k_raw[:, g, i + t, :].bitcast(F32), ident_f32[:])
+            nc.scalar.copy(
+                out=k_t[:, :, i * P : (i + 2) * P].rearrange("p g (t k) -> p g t k", t=2),
+                in_=bank[:],
+            )
+
+        items = []
+        first_item = []
+        last_item = []
+        for i in range(Q_TILES):
+            first_item.append(len(items))
+            for g in range(KV):
+                if i < 4:
+                    items.append((i, g, [0, 1], [0]))
+                else:
+                    items.append((i, g, [0], [0, 1]))
+                    items.append((i, g, [1], [0, 1]))
+            last_item.append(len(items) - 1)
+        live = {}
+
+        def scores_and_maxima(j):
+            i, g, heads, chunks = items[j]
+            keys = (i + 1) * P
+            banks = []
+            maxima = small.tile([P, 2], F32, name="maxima")
+            for h in heads:
+                for c in chunks:
+                    width = min(K_PASS, keys - c * K_PASS)
+                    s = psum_s.tile([P, BANK], F32, name="s")
+                    diagonal = c == chunks[-1]
+                    for e in range(2):
+                        nc.tensor.matmul(
+                            s[:, :width],
+                            lhsT=halves(q_t[:, i, g * PAIR + h, :])[:, :, e],
+                            rhs=halves(k_t[:, g, c * K_PASS : c * K_PASS + width])[:, :, e],
+                            start=(e == 0),
+                            stop=(e == 1 and not diagonal),
+                        )
+                    if diagonal:
+                        nc.tensor.matmul(
+                            s[:, width - P : width], lhsT=ident_bf[:], rhs=mask_bf[:], start=False, stop=True
+                        )
+                    piece = len(banks)
+                    nc.vector.tensor_reduce(out=maxima[:, piece : piece + 1], in_=s[:, :width], axis=AXIS_X, op=ALU.max)
+                    banks.append((s, width))
+            bias = small.tile([P, 2], F32, name="bias")
+            if len(chunks) == 2:
+                nc.vector.tensor_scalar(
+                    out=bias[:, 0:1], in0=maxima[:, 0:1], scalar1=maxima[:, 1:2], scalar2=neg_scale[:, 0:1],
+                    op0=ALU.max, op1=ALU.mult,
+                )
+            else:
+                nc.vector.tensor_scalar(
+                    out=bias[:], in0=maxima[:], scalar1=neg_scale[:, 0:1], scalar2=None, op0=ALU.mult
+                )
+            live[j] = {"banks": banks, "bias": bias}
+
+        def exponentials(j):
+            i, g, heads, chunks = items[j]
+            row_sums = small.tile([P, 2], F32, name="row_sums")
+            piece = 0
+            for h in heads:
+                for c in chunks:
+                    s, width = live[j]["banks"][piece]
+                    nc.scalar.activation(
+                        out=e_tiles[i][:, g * PAIR + h, c * K_PASS : c * K_PASS + width],
+                        in_=s[:, :width],
+                        func=FUNC.Exp,
+                        bias=live[j]["bias"][:, heads.index(h) : heads.index(h) + 1],
+                        scale=scale[:, 0:1],
+                        accum_out=row_sums[:, piece : piece + 1],
+                    )
+                    piece += 1
+            live[j]["row_sums"] = row_sums
+
+        def transpose_e(j):
+            i, g, heads, chunks = items[j]
+            bank = psum_t.tile([P, 2, 2, P], F32, name="bank_e", tag="t")
+            piece = 0
+            for h in heads:
+                for c in chunks:
+                    for u in range(2):
+                        first_key = c * K_PASS + u * HALF
+                        nc.tensor.transpose(
+                            bank[:, piece, u, :],
+                            e_tiles[i][:, g * PAIR + h, first_key : first_key + HALF].bitcast(F32),
+                            ident_f32[:],
+                        )
+                    piece += 1
+            e_grouped = work.tile([P, 2 * P * 2], F32, name="e_grouped", align_bytes=64)
+            nc.scalar.copy(
+                out=e_grouped[:].rearrange("p (s q u) -> p s q u", s=2, u=2),
+                in_=bank[:].rearrange("p s u q -> p s q u"),
+            )
+            live[j]["e_grouped"] = e_grouped
+
+        def quantise_e(j):
+            e_codes = work.tile([P, 2 * P], U32, name="e_codes", align_bytes=64)
+            e_scales = work.tile([P, 2 * P], U8, name="e_scales", align_bytes=64)
+            nc.vector.quantize_mx(
+                out=e_codes[:].bitcast(FP8X4), scales=e_scales[:], in_=live[j]["e_grouped"][:].bitcast(BF16)
+            )
+            live[j]["e_codes"] = e_codes
+            live[j]["e_scales"] = e_scales
+
+        def multiply_v_and_normalise(j):
+            i, g, heads, chunks = items[j]
+            row_sums = live[j]["row_sums"]
+            inverse = small.tile([P, 2], F32, name="inverse")
+            if len(chunks) == 2:
+                total = small.tile([P, 1], F32, name="total")
+                nc.vector.tensor_reduce(out=total[:], in_=row_sums[:], axis=AXIS_X, op=ALU.add)
+                nc.vector.reciprocal(out=inverse[:, 0:1], in_=total[:])
+            else:
+                nc.vector.reciprocal(out=inverse[:], in_=row_sums[:])
+            o = psum_acc.tile([P, 2, HD], F32, name="o", tag="acc")
+            piece = 0
+            for h in heads:
+                for c in chunks:
+                    v_cols = slice((g * 2 + c) * HD, (g * 2 + c + 1) * HD)
+                    nc.tensor.matmul_mx(
+                        out=o[:, heads.index(h), :],
+                        lhsT=live[j]["e_codes"][:, piece * P : (piece + 1) * P].bitcast(FP8X4),
+                        lhsT_scale=live[j]["e_scales"][:, piece * P : (piece + 1) * P],
+                        rhs=v_codes[:, v_cols].bitcast(FP8X4),
+                        rhs_scale=v_scales[:, v_cols],
+                        start=(c == chunks[0]),
+                        stop=(c == chunks[-1]),
+                    )
+                    piece += 1
+            for h in heads:
+                n = g * PAIR + h
+                nc.scalar.activation(
+                    out=a_tiles[i][:, n * HD : (n + 1) * HD],
+                    in_=o[:, heads.index(h), :],
+                    func=FUNC.Copy,
+                    scale=inverse[:, heads.index(h) : heads.index(h) + 1],
+                )
+
+        projecting = {}
+
+        def transpose_a(i):
+            bank = psum_t.tile([P, 2, 2, P], F32, name="bank_a", tag="t")
+            for g in range(2):
+                for u in range(2):
+                    first = g * K_PASS + u * HALF
+                    nc.tensor.transpose(bank[:, g, u, :], a_tiles[i][:, first : first + HALF].bitcast(F32), ident_f32[:])
+            a_grouped = work.tile([P, 2 * P * 2], F32, name="a_grouped", align_bytes=64)
+            nc.scalar.copy(
+                out=a_grouped[:].rearrange("p (g q u) -> p g q u", g=2, u=2),
+                in_=bank[:].rearrange("p g u q -> p g q u"),
+            )
+            projecting[i] = {"a_grouped": a_grouped}
+
+        def quantise_a(i):
+            a_codes = work.tile([P, 2 * P], U32, name="a_codes", align_bytes=64)
+            a_scales = work.tile([P, 2 * P], U8, name="a_scales", align_bytes=64)
+            nc.vector.quantize_mx(
+                out=a_codes[:].bitcast(FP8X4), scales=a_scales[:], in_=projecting[i]["a_grouped"][:].bitcast(BF16)
+            )
+            projecting[i]["a_codes"] = a_codes
+            projecting[i]["a_scales"] = a_scales
+            projecting[i]["result"] = work.tile([P, D], F32, name="result")
+
+        def project(i, half):
+            acc = psum_acc.tile([P, BANK], F32, name="acc", tag="acc")
+            for g in range(2):
+                w_cols = slice(g * D + half * BANK, g * D + (half + 1) * BANK)
+                nc.tensor.matmul_mx(
+                    out=acc[:],
+                    lhsT=projecting[i]["a_codes"][:, g * P : (g + 1) * P].bitcast(FP8X4),
+                    lhsT_scale=projecting[i]["a_scales"][:, g * P : (g + 1) * P],
+                    rhs=wo_codes[:, w_cols].bitcast(FP8X4),
+                    rhs_scale=wo_scales[:, w_cols],
+                    start=(g == 0),
+                    stop=(g == 1),
+                )
+            cols = slice(half * BANK, (half + 1) * BANK)
+            result = projecting[i]["result"]
+            nc.vector.scalar_tensor_tensor(
+                out=result[:, cols], in0=acc[:], scalar=gate_f[:, 0:1], in1=x_sb[:, i, cols], op0=ALU.mult, op1=ALU.add
+            )
+            if half == 1:
+                nc.sync.dma_start(out=out[0, i * P : (i + 1) * P, :], in_=result[:])
+
+        project_slot = [
+            max(last_item[i] + PROJECT_LAG, WO_FIRST_SLOT + 5 + 2 * i) for i in range(Q_TILES)
+        ]
+        transpose_k(0)
+        transpose_q(0)
+        for slot in range(-1, project_slot[-1] + 3):
+            if 0 <= slot - 2 < len(items):
+                quantise_e(slot - 2)
+            if slot - 1 in project_slot:
+                quantise_a(project_slot.index(slot - 1))
+            if 0 <= slot + 1 < len(items):
+                scores_and_maxima(slot + 1)
+            if 0 <= slot < len(items):
+                exponentials(slot)
+            if 0 <= slot - 1 < len(items):
+                transpose_e(slot - 1)
+            if slot in first_item and first_item.index(slot) + 1 < Q_TILES:
+                transpose_q(first_item.index(slot) + 1)
+            if slot - 1 in first_item and first_item.index(slot - 1) % 2 == 0 and first_item.index(slot - 1) + 2 < Q_TILES:
+                transpose_k(first_item.index(slot - 1) + 2)
+            if slot in project_slot:
+                transpose_a(project_slot.index(slot))
+            if 0 <= slot - 2 < len(items):
+                multiply_v_and_normalise(slot - 2)
+            if slot - 1 in project_slot:
+                project(project_slot.index(slot - 1), 0)
+            if slot - 2 in project_slot:
+                project(project_slot.index(slot - 2), 1)
+            if 0 <= slot - WO_FIRST_SLOT < 4:
+                regroup_wo(slot - WO_FIRST_SLOT)
+            if 0 <= slot - WO_FIRST_SLOT - 1 < 4:
+                quantise_wo(slot - WO_FIRST_SLOT - 1)
+            if slot == 0:
+                prepare_v(0)
+            if slot == V_SECOND_SLOT:
+                prepare_v(1)

@@ -41,7 +41,6 @@ def tile_sharedglobalattention_pb_kernel(tc, q_n, k_n, v, Wo, x, gate, log_tempe
         psum_s = ctx.enter_context(tc.psum_pool(name="psum_s", bufs=4))
         psum_t = ctx.enter_context(tc.psum_pool(name="psum_t", bufs=2))
         psum_acc = ctx.enter_context(tc.psum_pool(name="psum_acc", bufs=2))
-        ctx.enter_context(tc.manual_schedule())
 
         q_raw = resident.tile([P, Q_TILES, H, HD], BF16, name="q_raw")
         k_raw = resident.tile([P, KV, Q_TILES, HD], BF16, name="k_raw")

@@ -25,7 +25,7 @@ BANK = 512
 HALF = 256
 MASKED = -1.0e30
 WO_FIRST_SLOT = 4
-V_SECOND_SLOT = 6
+V_SECOND_SLOT = 3
 PROJECT_LAG = 3
 
 FLOPS = 2 * H * (512 * 512 + 512 * 1024) * HD * 2 + 2 * L * D * D
@@ -101,9 +101,9 @@ def tile_sharedglobalattention_pb_kernel(tc, q_n, k_n, v, Wo, x, gate, log_tempe
         load_k(2)
         load_q(2)
         load_q(3)
+        load_v(1)
         load_wo()
         load_k(4)
-        load_v(1)
         for i in range(4, Q_TILES):
             if i == 6:
                 load_k(i)
@@ -132,7 +132,8 @@ def tile_sharedglobalattention_pb_kernel(tc, q_n, k_n, v, Wo, x, gate, log_tempe
         for i in range(Q_TILES):
             keys = (i + 1) * P
             if keys < K_PASS * (i // 4 + 1):
-                nc.gpsimd.memset(e_tiles[i][:, :, keys:], 0.0)
+                words = e_tiles[i][:].rearrange("p h k -> p (h k)").bitcast(F32).rearrange("p (h w) -> p h w", h=H)
+                nc.vector.memset(words[:, :, keys // 2 :], 0.0)
 
         scale = const.tile([P, 1], F32, name="scale")
         nc.scalar.activation(out=scale[:], in_=lt_bf[:], func=FUNC.Exp)
@@ -366,8 +367,7 @@ def tile_sharedglobalattention_pb_kernel(tc, q_n, k_n, v, Wo, x, gate, log_tempe
             nc.vector.scalar_tensor_tensor(
                 out=result[:, cols], in0=acc[:], scalar=gate_f[:, 0:1], in1=x_sb[:, i, cols], op0=ALU.mult, op1=ALU.add
             )
-            if half == 1:
-                nc.sync.dma_start(out=out[0, i * P : (i + 1) * P, :], in_=result[:])
+            nc.sync.dma_start(out=out[0, i * P : (i + 1) * P, cols], in_=result[:, cols])
 
         project_slot = [
             max(last_item[i] + PROJECT_LAG, WO_FIRST_SLOT + 5 + 2 * i) for i in range(Q_TILES)

@@ -24,9 +24,13 @@ K_PASS = 512
 BANK = 512
 HALF = 256
 MASKED = -1.0e30
-WO_FIRST_SLOT = 4
+WO_GPSIMD = 3
+WO_VECTOR = 4
+WO_QUANT = [7, 9, 8, 12]
+PROJECT_FIRST = 11
 V_SECOND_SLOT = 3
-PROJECT_LAG = 3
+LAG_V = 3
+PROJECT_LAG = 4
 
 FLOPS = 2 * H * (512 * 512 + 512 * 1024) * HD * 2 + 2 * L * D * D
 
@@ -34,10 +38,11 @@ FLOPS = 2 * H * (512 * 512 + 512 * 1024) * HD * 2 + 2 * L * D * D
 def tile_sharedglobalattention_pb_kernel(tc, q_n, k_n, v, Wo, x, gate, log_temperature, out):
     nc = tc.nc
     with ExitStack() as ctx:
+        ctx.enter_context(tc.manual_schedule())
         const = ctx.enter_context(tc.tile_pool(name="const", bufs=1))
         resident = ctx.enter_context(tc.tile_pool(name="resident", bufs=1))
-        work = ctx.enter_context(tc.tile_pool(name="work", bufs=3))
-        small = ctx.enter_context(tc.tile_pool(name="small", bufs=4))
+        work = ctx.enter_context(tc.tile_pool(name="work", bufs=4))
+        small = ctx.enter_context(tc.tile_pool(name="small", bufs=6))
         psum_s = ctx.enter_context(tc.psum_pool(name="psum_s", bufs=4))
         psum_t = ctx.enter_context(tc.psum_pool(name="psum_t", bufs=2))
         psum_acc = ctx.enter_context(tc.psum_pool(name="psum_acc", bufs=2))
@@ -61,19 +66,17 @@ def tile_sharedglobalattention_pb_kernel(tc, q_n, k_n, v, Wo, x, gate, log_tempe
 
         lt_bf = const.tile([P, 1], BF16, name="lt_bf")
         gate_bf = const.tile([P, 1], BF16, name="gate_bf")
-        nc.sync.dma_start(out=lt_bf[:], in_=log_temperature.partition_broadcast(P))
-        nc.sync.dma_start(out=gate_bf[:], in_=gate.partition_broadcast(P))
 
-        def load_k(i):
-            for g in range(KV):
+        def load_k(i, groups=range(KV)):
+            for g in groups:
                 nc.sync.dma_start(
                     out=k_raw[:, g, i : i + 2, :],
                     in_=k_n[0, g, i * P : (i + 2) * P, :].rearrange("(t p) d -> p t d", p=P),
                 )
 
-        def load_q(i):
+        def load_q(i, heads=slice(0, H)):
             nc.sync.dma_start(
-                out=q_raw[:, i, :, :], in_=q_n[0, :, i * P : (i + 1) * P, :].rearrange("n p d -> p n d")
+                out=q_raw[:, i, heads, :], in_=q_n[0, heads, i * P : (i + 1) * P, :].rearrange("n p d -> p n d")
             )
 
         def load_v(c):
@@ -94,24 +97,39 @@ def tile_sharedglobalattention_pb_kernel(tc, q_n, k_n, v, Wo, x, gate, log_tempe
         def load_x(i):
             nc.sync.dma_start(out=x_sb[:, i, :], in_=x[0, i * P : (i + 1) * P, :])
 
-        load_k(0)
-        load_q(0)
-        load_v(0)
+        for g in range(KV):
+            load_k(0, [g])
+            load_q(0, slice(g * PAIR, (g + 1) * PAIR))
+        nc.sync.dma_start(out=lt_bf[:], in_=log_temperature.partition_broadcast(P))
         load_q(1)
         load_k(2)
+        load_v(0)
         load_q(2)
         load_q(3)
-        load_v(1)
-        load_wo()
         load_k(4)
-        for i in range(4, Q_TILES):
-            if i == 6:
-                load_k(i)
-            load_q(i)
-            load_x(i - 4)
+        load_q(4)
+        load_v(1)
+        nc.sync.dma_start(out=gate_bf[:], in_=gate.partition_broadcast(P))
+        load_wo()
+        load_q(5)
+        load_x(0)
+        load_k(6)
+        load_q(6)
+        load_x(1)
+        load_q(7)
+        load_x(2)
+        load_x(3)
         for i in range(4, Q_TILES):
             load_x(i)
 
+        warm = const.tile([P, 1], F32, name="warm")
+        nc.vector.memset(warm[:], 0.0)
+        nc.scalar.activation(out=warm[:], in_=warm[:], func=FUNC.Exp)
+        for i in range(Q_TILES):
+            keys = (i + 1) * P
+            if keys < K_PASS * (i // 4 + 1):
+                words = e_tiles[i][:].rearrange("p h k -> p (h k)").bitcast(F32).rearrange("p (h w) -> p h w", h=H)
+                nc.vector.memset(words[:, :, keys // 2 :], 0.0)
         ident_f32 = const.tile([P, P], F32, name="ident_f32")
         make_identity(nc, ident_f32[:])
         ident_bf = const.tile([P, P], BF16, name="ident_bf")
@@ -129,44 +147,48 @@ def tile_sharedglobalattention_pb_kernel(tc, q_n, k_n, v, Wo, x, gate, log_tempe
         )
         mask_bf = const.tile([P, P], BF16, name="mask_bf")
         nc.vector.tensor_copy(out=mask_bf[:], in_=mask_f32[:])
-        for i in range(Q_TILES):
-            keys = (i + 1) * P
-            if keys < K_PASS * (i // 4 + 1):
-                words = e_tiles[i][:].rearrange("p h k -> p (h k)").bitcast(F32).rearrange("p (h w) -> p h w", h=H)
-                nc.vector.memset(words[:, :, keys // 2 :], 0.0)
-
         scale = const.tile([P, 1], F32, name="scale")
-        nc.scalar.activation(out=scale[:], in_=lt_bf[:], func=FUNC.Exp)
         neg_scale = const.tile([P, 1], F32, name="neg_scale")
-        nc.vector.tensor_scalar(out=neg_scale[:], in0=scale[:], scalar1=-1.0, scalar2=None, op0=ALU.mult)
+        minus_one = const.tile([P, 2], F32, name="minus_one")
+        nc.gpsimd.memset(minus_one[:], -1.0)
         gate_f = const.tile([P, 1], F32, name="gate_f")
-        nc.vector.tensor_copy(out=gate_f[:], in_=gate_bf[:])
 
-        def regroup(raw, width):
-            grouped = work.tile([P, 4 * BANK], BF16, name="grouped", align_bytes=64)
+        def regroup(grouped, raw):
             nc.vector.tensor_copy(
-                out=grouped[:, : 4 * width].rearrange("p (c i t) -> p c t i", i=4, t=4),
-                in_=raw.rearrange("p t (c i) -> p c t i", i=4),
+                out=grouped.rearrange("p (c i t) -> p c t i", i=4, t=4), in_=raw.rearrange("p t (c i) -> p c t i", i=4)
             )
-            return grouped
 
-        def prepare_v(c):
-            grouped = []
+        def regroup_on_gpsimd(grouped, raw):
+            nc.gpsimd.tensor_scalar(
+                out=grouped.rearrange("p (c i t) -> p c t i", i=4, t=4), in0=raw.rearrange("p t (c i) -> p c t i", i=4),
+                scalar1=1.0, scalar2=0.0, op0=ALU.mult, op1=ALU.add,
+            )
+
+        v_grouped = {}
+
+        def regroup_v(c):
             for g in range(KV):
                 cols = slice((g * 2 + c) * 4 * HD, (g * 2 + c + 1) * 4 * HD)
-                grouped.append(regroup(v_raw[:, cols].rearrange("p (t d) -> p t d", t=4), HD))
+                v_grouped[g] = work.tile([P, 4 * HD], BF16, name="v_grouped", align_bytes=64)
+                regroup(v_grouped[g][:], v_raw[:, cols].rearrange("p (t d) -> p t d", t=4))
+
+        def quantise_v(c):
             for g in range(KV):
                 cols = slice((g * 2 + c) * HD, (g * 2 + c + 1) * HD)
                 nc.vector.quantize_mx(
-                    out=v_codes[:, cols].bitcast(FP8X4), scales=v_scales[:, cols], in_=grouped[g][:, : 4 * HD]
+                    out=v_codes[:, cols].bitcast(FP8X4), scales=v_scales[:, cols], in_=v_grouped[g][:]
                 )
 
-        wo_grouped = {}
+        wo_grouped = [resident.tile([P, 4 * BANK], BF16, name="wo_grouped%d" % w, align_bytes=64) for w in range(4)]
 
-        def regroup_wo(w):
+        def regroup_wo(w, part, parts, form):
             g, half = w // 2, w % 2
             raw = wo_raw[:, g * 4 * D : (g + 1) * 4 * D].rearrange("p (t n) -> p t n", t=4)
-            wo_grouped[w] = regroup(raw[:, :, half * BANK : (half + 1) * BANK], BANK)
+            width = BANK // parts
+            form(
+                wo_grouped[w][:, part * 4 * width : (part + 1) * 4 * width],
+                raw[:, :, half * BANK + part * width : half * BANK + (part + 1) * width],
+            )
 
         def quantise_wo(w):
             cols = slice(w * BANK, (w + 1) * BANK)
@@ -174,6 +196,17 @@ def tile_sharedglobalattention_pb_kernel(tc, q_n, k_n, v, Wo, x, gate, log_tempe
 
         def halves(words):
             return words.bitcast(BF16).rearrange("p (c e) -> p c e", e=2)
+
+        def transpose_first(g):
+            pool, tag = ((psum_t, "t"), (psum_acc, "acc"))[g]
+            bank = pool.tile([P, 2, P], F32, name="bank_k0", tag=tag)
+            for t in range(2):
+                nc.tensor.transpose(bank[:, t, :], k_raw[:, g, t, :].bitcast(F32), ident_f32[:])
+            nc.scalar.copy(out=k_t[:, g, : 2 * P].rearrange("p (t k) -> p t k", t=2), in_=bank[:])
+            bank = pool.tile([P, PAIR, P], F32, name="bank_q0", tag=tag)
+            for h in range(PAIR):
+                nc.tensor.transpose(bank[:, h, :], q_raw[:, 0, g * PAIR + h, :].bitcast(F32), ident_f32[:])
+            nc.vector.tensor_copy(out=q_t[:, 0, g * PAIR : (g + 1) * PAIR, :], in_=bank[:])
 
         def transpose_q(i):
             bank = psum_t.tile([P, H, P], F32, name="bank_q", tag="t")
@@ -205,31 +238,30 @@ def tile_sharedglobalattention_pb_kernel(tc, q_n, k_n, v, Wo, x, gate, log_tempe
             last_item.append(len(items) - 1)
         live = {}
 
-        def scores_and_maxima(j):
+        def scores_and_maxima(j, piece):
             i, g, heads, chunks = items[j]
             keys = (i + 1) * P
-            banks = []
-            maxima = small.tile([P, 2], F32, name="maxima")
-            for h in heads:
-                for c in chunks:
-                    width = min(K_PASS, keys - c * K_PASS)
-                    s = psum_s.tile([P, BANK], F32, name="s")
-                    diagonal = c == chunks[-1]
-                    for e in range(2):
-                        nc.tensor.matmul(
-                            s[:, :width],
-                            lhsT=halves(q_t[:, i, g * PAIR + h, :])[:, :, e],
-                            rhs=halves(k_t[:, g, c * K_PASS : c * K_PASS + width])[:, :, e],
-                            start=(e == 0),
-                            stop=(e == 1 and not diagonal),
-                        )
-                    if diagonal:
-                        nc.tensor.matmul(
-                            s[:, width - P : width], lhsT=ident_bf[:], rhs=mask_bf[:], start=False, stop=True
-                        )
-                    piece = len(banks)
-                    nc.vector.tensor_reduce(out=maxima[:, piece : piece + 1], in_=s[:, :width], axis=AXIS_X, op=ALU.max)
-                    banks.append((s, width))
+            h, c = [(h, c) for h in heads for c in chunks][piece]
+            if piece == 0:
+                live[j] = {"banks": [], "maxima": small.tile([P, 2], F32, name="maxima")}
+            maxima = live[j]["maxima"]
+            width = min(K_PASS, keys - c * K_PASS)
+            s = psum_s.tile([P, BANK], F32, name="s")
+            diagonal = c == chunks[-1]
+            for e in range(2):
+                nc.tensor.matmul(
+                    s[:, :width],
+                    lhsT=halves(q_t[:, i, g * PAIR + h, :])[:, :, e],
+                    rhs=halves(k_t[:, g, c * K_PASS : c * K_PASS + width])[:, :, e],
+                    start=(e == 0),
+                    stop=(e == 1 and not diagonal),
+                )
+            if diagonal:
+                nc.tensor.matmul(s[:, width - P : width], lhsT=ident_bf[:], rhs=mask_bf[:], start=False, stop=True)
+            nc.vector.tensor_reduce(out=maxima[:, piece : piece + 1], in_=s[:, :width], axis=AXIS_X, op=ALU.max)
+            live[j]["banks"].append((s, width))
+            if piece == 0:
+                return
             bias = small.tile([P, 2], F32, name="bias")
             if len(chunks) == 2:
                 nc.vector.tensor_scalar(
@@ -240,7 +272,7 @@ def tile_sharedglobalattention_pb_kernel(tc, q_n, k_n, v, Wo, x, gate, log_tempe
                 nc.vector.tensor_scalar(
                     out=bias[:], in0=maxima[:], scalar1=neg_scale[:, 0:1], scalar2=None, op0=ALU.mult
                 )
-            live[j] = {"banks": banks, "bias": bias}
+            live[j]["bias"] = bias
 
         def exponentials(j):
             i, g, heads, chunks = items[j]
@@ -290,16 +322,20 @@ def tile_sharedglobalattention_pb_kernel(tc, q_n, k_n, v, Wo, x, gate, log_tempe
             live[j]["e_codes"] = e_codes
             live[j]["e_scales"] = e_scales
 
-        def multiply_v_and_normalise(j):
+        def invert_row_sums(j):
             i, g, heads, chunks = items[j]
             row_sums = live[j]["row_sums"]
             inverse = small.tile([P, 2], F32, name="inverse")
             if len(chunks) == 2:
                 total = small.tile([P, 1], F32, name="total")
-                nc.vector.tensor_reduce(out=total[:], in_=row_sums[:], axis=AXIS_X, op=ALU.add)
-                nc.vector.reciprocal(out=inverse[:, 0:1], in_=total[:])
+                nc.gpsimd.tensor_tensor(out=total[:], in0=row_sums[:, 0:1], in1=row_sums[:, 1:2], op=ALU.add)
+                nc.gpsimd.tensor_tensor(out=inverse[:, 0:1], in0=total[:], in1=minus_one[:, 0:1], op=ALU.pow)
             else:
-                nc.vector.reciprocal(out=inverse[:], in_=row_sums[:])
+                nc.gpsimd.tensor_tensor(out=inverse[:], in0=row_sums[:], in1=minus_one[:], op=ALU.pow)
+            live[j]["inverse"] = inverse
+
+        def multiply_v(j):
+            i, g, heads, chunks = items[j]
             o = psum_acc.tile([P, 2, HD], F32, name="o", tag="acc")
             piece = 0
             for h in heads:
@@ -315,6 +351,11 @@ def tile_sharedglobalattention_pb_kernel(tc, q_n, k_n, v, Wo, x, gate, log_tempe
                         stop=(c == chunks[-1]),
                     )
                     piece += 1
+            live[j]["o"] = o
+
+        def normalise(j):
+            i, g, heads, chunks = items[j]
+            o, inverse = live[j]["o"], live[j]["inverse"]
             for h in heads:
                 n = g * PAIR + h
                 nc.scalar.activation(
@@ -370,38 +411,57 @@ def tile_sharedglobalattention_pb_kernel(tc, q_n, k_n, v, Wo, x, gate, log_tempe
             nc.sync.dma_start(out=out[0, i * P : (i + 1) * P, cols], in_=result[:, cols])
 
         project_slot = [
-            max(last_item[i] + PROJECT_LAG, WO_FIRST_SLOT + 5 + 2 * i) for i in range(Q_TILES)
+            max(last_item[i] + PROJECT_LAG, PROJECT_FIRST + 2 * i) for i in range(Q_TILES)
         ]
-        transpose_k(0)
-        transpose_q(0)
-        for slot in range(-1, project_slot[-1] + 3):
+        transpose_first(0)
+        transpose_first(1)
+        nc.scalar.activation(out=scale[:], in_=lt_bf[:], func=FUNC.Exp)
+        nc.vector.tensor_scalar(out=neg_scale[:], in0=scale[:], scalar1=-1.0, scalar2=None, op0=ALU.mult)
+        scores_and_maxima(0, 0)
+        scores_and_maxima(0, 1)
+        transpose_q(1)
+        for slot in range(0, project_slot[-1] + 3):
             if 0 <= slot - 2 < len(items):
                 quantise_e(slot - 2)
             if slot - 1 in project_slot:
                 quantise_a(project_slot.index(slot - 1))
             if 0 <= slot + 1 < len(items):
-                scores_and_maxima(slot + 1)
+                scores_and_maxima(slot + 1, 0)
             if 0 <= slot < len(items):
                 exponentials(slot)
+                invert_row_sums(slot)
             if 0 <= slot - 1 < len(items):
                 transpose_e(slot - 1)
-            if slot in first_item and first_item.index(slot) + 1 < Q_TILES:
-                transpose_q(first_item.index(slot) + 1)
-            if slot - 1 in first_item and first_item.index(slot - 1) % 2 == 0 and first_item.index(slot - 1) + 2 < Q_TILES:
-                transpose_k(first_item.index(slot - 1) + 2)
+            if slot + 3 in first_item and first_item.index(slot + 3) >= 2:
+                transpose_q(first_item.index(slot + 3))
+            if slot + 4 in first_item and first_item.index(slot + 4) % 2 == 0:
+                transpose_k(first_item.index(slot + 4))
             if slot in project_slot:
                 transpose_a(project_slot.index(slot))
-            if 0 <= slot - 2 < len(items):
-                multiply_v_and_normalise(slot - 2)
+            if 0 <= slot + 1 < len(items):
+                scores_and_maxima(slot + 1, 1)
+            if 0 <= slot - LAG_V < len(items):
+                multiply_v(slot - LAG_V)
+                normalise(slot - LAG_V)
             if slot - 1 in project_slot:
                 project(project_slot.index(slot - 1), 0)
             if slot - 2 in project_slot:
                 project(project_slot.index(slot - 2), 1)
-            if 0 <= slot - WO_FIRST_SLOT < 4:
-                regroup_wo(slot - WO_FIRST_SLOT)
-            if 0 <= slot - WO_FIRST_SLOT - 1 < 4:
-                quantise_wo(slot - WO_FIRST_SLOT - 1)
+            if 0 <= slot - WO_GPSIMD < 8:
+                w = 2 + (slot - WO_GPSIMD) // 4
+                regroup_wo(w, (slot - WO_GPSIMD) % 4, 4, regroup_on_gpsimd)
+            if 0 <= slot - WO_VECTOR < 4:
+                w = (slot - WO_VECTOR) // 2
+                regroup_wo(w, (slot - WO_VECTOR) % 2, 2, regroup)
+            for w in range(4):
+                if slot == WO_QUANT[w]:
+                    quantise_wo(w)
             if slot == 0:
-                prepare_v(0)
+                regroup_v(0)
+            if slot == 2:
+                quantise_v(0)
             if slot == V_SECOND_SLOT:
-                prepare_v(1)
+                regroup_v(1)
+                nc.vector.tensor_copy(out=gate_f[:], in_=gate_bf[:])
+            if slot == V_SECOND_SLOT + 2:
+                quantise_v(1)

@@ -30,7 +30,10 @@ WO_QUANT = [7, 9, 8, 12]
 PROJECT_FIRST = 11
 V_SECOND_SLOT = 3
 LAG_V = 3
-PROJECT_LAG = 4
+ORDER = [0, 1, 2, 3, 4, 5, 6, 7]
+PROJECT_STEP = 2
+AHEAD = 5
+LOADS = [(a[0], int(a[1])) for a in "q1 k2 v0 q2 q3 k4 q4 v1 g0 w0 q5 x0 k6 q6 x1 q7 x2 x3 x4 x5 x6 x7".split()]
 
 FLOPS = 2 * H * (512 * 512 + 512 * 1024) * HD * 2 + 2 * L * D * D
 
@@ -87,7 +90,7 @@ def tile_sharedglobalattention_pb_kernel(tc, q_n, k_n, v, Wo, x, gate, log_tempe
                     in_=v[0, g, c * K_PASS : (c + 1) * K_PASS, :].rearrange("(u p e) d -> p u e d", p=P, e=2),
                 )
 
-        def load_wo():
+        def load_wo(i):
             for g in range(2):
                 nc.sync.dma_start(
                     out=wo_raw[:, g * 4 * D : (g + 1) * 4 * D].rearrange("p (u e n) -> p u e n", e=2, n=D),
@@ -99,28 +102,13 @@ def tile_sharedglobalattention_pb_kernel(tc, q_n, k_n, v, Wo, x, gate, log_tempe
 
         for g in range(KV):
             load_k(0, [g])
-            load_q(0, slice(g * PAIR, (g + 1) * PAIR))
+            load_q(ORDER[0], slice(g * PAIR, (g + 1) * PAIR))
         nc.sync.dma_start(out=lt_bf[:], in_=log_temperature.partition_broadcast(P))
-        load_q(1)
-        load_k(2)
-        load_v(0)
-        load_q(2)
-        load_q(3)
-        load_k(4)
-        load_q(4)
-        load_v(1)
-        nc.sync.dma_start(out=gate_bf[:], in_=gate.partition_broadcast(P))
-        load_wo()
-        load_q(5)
-        load_x(0)
-        load_k(6)
-        load_q(6)
-        load_x(1)
-        load_q(7)
-        load_x(2)
-        load_x(3)
-        for i in range(4, Q_TILES):
-            load_x(i)
+        def load_gate(i):
+            nc.sync.dma_start(out=gate_bf[:], in_=gate.partition_broadcast(P))
+
+        for name, arg in LOADS:
+            {"q": load_q, "k": load_k, "v": load_v, "x": load_x, "w": load_wo, "g": load_gate}[name](arg)
 
         warm = const.tile([P, 1], F32, name="warm")
         nc.vector.memset(warm[:], 0.0)
@@ -205,8 +193,8 @@ def tile_sharedglobalattention_pb_kernel(tc, q_n, k_n, v, Wo, x, gate, log_tempe
             nc.scalar.copy(out=k_t[:, g, : 2 * P].rearrange("p (t k) -> p t k", t=2), in_=bank[:])
             bank = pool.tile([P, PAIR, P], F32, name="bank_q0", tag=tag)
             for h in range(PAIR):
-                nc.tensor.transpose(bank[:, h, :], q_raw[:, 0, g * PAIR + h, :].bitcast(F32), ident_f32[:])
-            nc.vector.tensor_copy(out=q_t[:, 0, g * PAIR : (g + 1) * PAIR, :], in_=bank[:])
+                nc.tensor.transpose(bank[:, h, :], q_raw[:, ORDER[0], g * PAIR + h, :].bitcast(F32), ident_f32[:])
+            nc.vector.tensor_copy(out=q_t[:, ORDER[0], g * PAIR : (g + 1) * PAIR, :], in_=bank[:])
 
         def transpose_q(i):
             bank = psum_t.tile([P, H, P], F32, name="bank_q", tag="t")
@@ -225,17 +213,17 @@ def tile_sharedglobalattention_pb_kernel(tc, q_n, k_n, v, Wo, x, gate, log_tempe
             )
 
         items = []
-        first_item = []
-        last_item = []
-        for i in range(Q_TILES):
-            first_item.append(len(items))
+        first_item = [0] * Q_TILES
+        last_item = [0] * Q_TILES
+        for i in ORDER:
+            first_item[i] = len(items)
             for g in range(KV):
                 if i < 4:
                     items.append((i, g, [0, 1], [0]))
                 else:
                     items.append((i, g, [0], [0, 1]))
                     items.append((i, g, [1], [0, 1]))
-            last_item.append(len(items) - 1)
+            last_item[i] = len(items) - 1
         live = {}
 
         def scores_and_maxima(j, piece):
@@ -410,43 +398,60 @@ def tile_sharedglobalattention_pb_kernel(tc, q_n, k_n, v, Wo, x, gate, log_tempe
             )
             nc.sync.dma_start(out=out[0, i * P : (i + 1) * P, cols], in_=result[:, cols])
 
-        project_slot = [
-            max(last_item[i] + PROJECT_LAG, PROJECT_FIRST + 2 * i) for i in range(Q_TILES)
-        ]
+        n_items = len(items)
+        other_run = {}
+        needs = [(first_item[i], "q", i) for i in ORDER[2:]]
+        for pair in range(2, Q_TILES, 2):
+            needs.append((min(first_item[i] for i in range(pair, Q_TILES)), "k", pair))
+        for need, kind, i in sorted(needs):
+            slot = max(need - AHEAD, 0)
+            while slot in other_run and slot > 0:
+                slot = slot - 1
+            while slot in other_run:
+                slot = slot + 1
+            other_run[slot] = (kind, i)
+        multiply_slot = [min(j + LAG_V, max(n_items + 1, j + 2)) for j in range(n_items)]
+        project_slot = {}
+        earliest = PROJECT_FIRST
+        for i in ORDER:
+            slot = max(multiply_slot[last_item[i]] + 1, earliest)
+            while slot in other_run:
+                slot = slot + 1
+            other_run[slot] = ("a", i)
+            project_slot[slot] = i
+            earliest = slot + PROJECT_STEP
         transpose_first(0)
         transpose_first(1)
         nc.scalar.activation(out=scale[:], in_=lt_bf[:], func=FUNC.Exp)
         nc.vector.tensor_scalar(out=neg_scale[:], in0=scale[:], scalar1=-1.0, scalar2=None, op0=ALU.mult)
         scores_and_maxima(0, 0)
         scores_and_maxima(0, 1)
-        transpose_q(1)
-        for slot in range(0, project_slot[-1] + 3):
-            if 0 <= slot - 2 < len(items):
+        transpose_q(ORDER[1])
+        for slot in range(0, max(project_slot) + 3):
+            if 0 <= slot - 2 < n_items:
                 quantise_e(slot - 2)
             if slot - 1 in project_slot:
-                quantise_a(project_slot.index(slot - 1))
-            if 0 <= slot + 1 < len(items):
+                quantise_a(project_slot[slot - 1])
+            if slot + 1 < n_items:
                 scores_and_maxima(slot + 1, 0)
-            if 0 <= slot < len(items):
+            if slot < n_items:
                 exponentials(slot)
                 invert_row_sums(slot)
-            if 0 <= slot - 1 < len(items):
+            if 0 <= slot - 1 < n_items:
                 transpose_e(slot - 1)
-            if slot + 3 in first_item and first_item.index(slot + 3) >= 2:
-                transpose_q(first_item.index(slot + 3))
-            if slot + 4 in first_item and first_item.index(slot + 4) % 2 == 0:
-                transpose_k(first_item.index(slot + 4))
-            if slot in project_slot:
-                transpose_a(project_slot.index(slot))
-            if 0 <= slot + 1 < len(items):
+            if slot in other_run:
+                kind, i = other_run[slot]
+                {"q": transpose_q, "k": transpose_k, "a": transpose_a}[kind](i)
+            if slot + 1 < n_items:
                 scores_and_maxima(slot + 1, 1)
-            if 0 <= slot - LAG_V < len(items):
-                multiply_v(slot - LAG_V)
-                normalise(slot - LAG_V)
+            for j in range(n_items):
+                if slot == multiply_slot[j]:
+                    multiply_v(j)
+                    normalise(j)
             if slot - 1 in project_slot:
-                project(project_slot.index(slot - 1), 0)
+                project(project_slot[slot - 1], 0)
             if slot - 2 in project_slot:
-                project(project_slot.index(slot - 2), 1)
+                project(project_slot[slot - 2], 1)
             if 0 <= slot - WO_GPSIMD < 8:
                 w = 2 + (slot - WO_GPSIMD) // 4
                 regroup_wo(w, (slot - WO_GPSIMD) % 4, 4, regroup_on_gpsimd)

@@ -25,7 +25,7 @@ BANK = 512
 HALF = 256
 MASKED = -1.0e30
 WO_GPSIMD = 3
-WO_VECTOR = 4
+WO_VECTOR = 5
 WO_QUANT = [7, 9, 8, 12]
 PROJECT_FIRST = 11
 V_SECOND_SLOT = 3
@@ -224,6 +224,7 @@ def tile_sharedglobalattention_pb_kernel(tc, q_n, k_n, v, Wo, x, gate, log_tempe
                     items.append((i, g, [0], [0, 1]))
                     items.append((i, g, [1], [0, 1]))
             last_item[i] = len(items) - 1
+        n_items = len(items)
         live = {}
 
         def scores_and_maxima(j, piece):
@@ -280,35 +281,47 @@ def tile_sharedglobalattention_pb_kernel(tc, q_n, k_n, v, Wo, x, gate, log_tempe
                     piece += 1
             live[j]["row_sums"] = row_sums
 
-        def transpose_e(j):
-            i, g, heads, chunks = items[j]
-            bank = psum_t.tile([P, 2, 2, P], F32, name="bank_e", tag="t")
-            piece = 0
-            for h in heads:
-                for c in chunks:
-                    for u in range(2):
-                        first_key = c * K_PASS + u * HALF
-                        nc.tensor.transpose(
-                            bank[:, piece, u, :],
-                            e_tiles[i][:, g * PAIR + h, first_key : first_key + HALF].bitcast(F32),
-                            ident_f32[:],
-                        )
-                    piece += 1
-            e_grouped = work.tile([P, 2 * P * 2], F32, name="e_grouped", align_bytes=64)
-            nc.scalar.copy(
-                out=e_grouped[:].rearrange("p (s q u) -> p s q u", s=2, u=2),
-                in_=bank[:].rearrange("p s u q -> p s q u"),
-            )
-            live[j]["e_grouped"] = e_grouped
+        def transpose_bank(n, draining):
+            if draining:
+                return psum_s.tile([P, n, 2, P], F32, name="bank_drain", tag="s")
+            return psum_t.tile([P, n, 2, P], F32, name="bank", tag="t")
 
-        def quantise_e(j):
-            e_codes = work.tile([P, 2 * P], U32, name="e_codes", align_bytes=64)
-            e_scales = work.tile([P, 2 * P], U8, name="e_scales", align_bytes=64)
+        def copy_out(grouped, bank, n, on_vector):
+            out, in_ = grouped.rearrange("p (s q u) -> p s q u", s=n, u=2), bank[:].rearrange("p s u q -> p s q u")
+            if on_vector:
+                nc.vector.tensor_copy(out=out, in_=in_)
+            else:
+                nc.scalar.copy(out=out, in_=in_)
+
+        def transpose_e(j, pieces=(0, 1), draining=False):
+            i, g, heads, chunks = items[j]
+            n_pieces = len(pieces)
+            bank = transpose_bank(n_pieces, draining)
+            for piece in pieces:
+                h, c = [(h, c) for h in heads for c in chunks][piece]
+                for u in range(2):
+                    first_key = c * K_PASS + u * HALF
+                    nc.tensor.transpose(
+                        bank[:, piece - pieces[0], u, :],
+                        e_tiles[i][:, g * PAIR + h, first_key : first_key + HALF].bitcast(F32),
+                        ident_f32[:],
+                    )
+            if pieces[0] == 0:
+                live[j]["e_grouped"] = work.tile([P, 2 * P * 2], F32, name="e_grouped", align_bytes=64)
+            words = live[j]["e_grouped"][:, pieces[0] * P * 2 : (pieces[-1] + 1) * P * 2]
+            copy_out(words, bank, n_pieces, j == n_items - 2)
+
+        def quantise_e(j, pieces=(0, 1)):
+            if pieces[0] == 0:
+                live[j]["e_codes"] = work.tile([P, 2 * P], U32, name="e_codes", align_bytes=64)
+                live[j]["e_scales"] = work.tile([P, 2 * P], U8, name="e_scales", align_bytes=64)
+            cols = slice(pieces[0] * P, (pieces[-1] + 1) * P)
+            words = live[j]["e_grouped"][:, pieces[0] * P * 2 : (pieces[-1] + 1) * P * 2]
             nc.vector.quantize_mx(
-                out=e_codes[:].bitcast(FP8X4), scales=e_scales[:], in_=live[j]["e_grouped"][:].bitcast(BF16)
+                out=live[j]["e_codes"][:, cols].bitcast(FP8X4),
+                scales=live[j]["e_scales"][:, cols],
+                in_=words.bitcast(BF16),
             )
-            live[j]["e_codes"] = e_codes
-            live[j]["e_scales"] = e_scales
 
         def invert_row_sums(j):
             i, g, heads, chunks = items[j]
@@ -322,9 +335,14 @@ def tile_sharedglobalattention_pb_kernel(tc, q_n, k_n, v, Wo, x, gate, log_tempe
                 nc.gpsimd.tensor_tensor(out=inverse[:], in0=row_sums[:], in1=minus_one[:], op=ALU.pow)
             live[j]["inverse"] = inverse
 
-        def multiply_v(j):
+        def accumulator(shape, draining):
+            if draining:
+                return psum_s.tile(shape, F32, name="acc_drain", tag="s")
+            return psum_acc.tile(shape, F32, name="acc", tag="acc")
+
+        def multiply_v(j, draining=False):
             i, g, heads, chunks = items[j]
-            o = psum_acc.tile([P, 2, HD], F32, name="o", tag="acc")
+            o = accumulator([P, 2, HD], draining)
             piece = 0
             for h in heads:
                 for c in chunks:
@@ -355,32 +373,38 @@ def tile_sharedglobalattention_pb_kernel(tc, q_n, k_n, v, Wo, x, gate, log_tempe
 
         projecting = {}
 
-        def transpose_a(i):
-            bank = psum_t.tile([P, 2, 2, P], F32, name="bank_a", tag="t")
-            for g in range(2):
+        def transpose_a(i, passes=(0, 1), draining=False):
+            n_passes = len(passes)
+            bank = transpose_bank(n_passes, draining)
+            for g in passes:
                 for u in range(2):
                     first = g * K_PASS + u * HALF
-                    nc.tensor.transpose(bank[:, g, u, :], a_tiles[i][:, first : first + HALF].bitcast(F32), ident_f32[:])
-            a_grouped = work.tile([P, 2 * P * 2], F32, name="a_grouped", align_bytes=64)
-            nc.scalar.copy(
-                out=a_grouped[:].rearrange("p (g q u) -> p g q u", g=2, u=2),
-                in_=bank[:].rearrange("p g u q -> p g q u"),
-            )
-            projecting[i] = {"a_grouped": a_grouped}
+                    nc.tensor.transpose(
+                        bank[:, g - passes[0], u, :], a_tiles[i][:, first : first + HALF].bitcast(F32), ident_f32[:]
+                    )
+            if passes[0] == 0:
+                projecting[i] = {"a_grouped": work.tile([P, 2 * P * 2], F32, name="a_grouped", align_bytes=64)}
+            words = projecting[i]["a_grouped"][:, passes[0] * P * 2 : (passes[-1] + 1) * P * 2]
+            copy_out(words, bank, n_passes, i == ORDER[-2])
 
-        def quantise_a(i):
-            a_codes = work.tile([P, 2 * P], U32, name="a_codes", align_bytes=64)
-            a_scales = work.tile([P, 2 * P], U8, name="a_scales", align_bytes=64)
+        def quantise_a(i, passes=(0, 1)):
+            if passes[0] == 0:
+                projecting[i]["a_codes"] = work.tile([P, 2 * P], U32, name="a_codes", align_bytes=64)
+                projecting[i]["a_scales"] = work.tile([P, 2 * P], U8, name="a_scales", align_bytes=64)
+                projecting[i]["result"] = work.tile([P, D], F32, name="result")
+            cols = slice(passes[0] * P, (passes[-1] + 1) * P)
+            words = projecting[i]["a_grouped"][:, passes[0] * P * 2 : (passes[-1] + 1) * P * 2]
             nc.vector.quantize_mx(
-                out=a_codes[:].bitcast(FP8X4), scales=a_scales[:], in_=projecting[i]["a_grouped"][:].bitcast(BF16)
+                out=projecting[i]["a_codes"][:, cols].bitcast(FP8X4),
+                scales=projecting[i]["a_scales"][:, cols],
+                in_=words.bitcast(BF16),
             )
-            projecting[i]["a_codes"] = a_codes
-            projecting[i]["a_scales"] = a_scales
-            projecting[i]["result"] = work.tile([P, D], F32, name="result")
 
-        def project(i, half):
-            acc = psum_acc.tile([P, BANK], F32, name="acc", tag="acc")
-            for g in range(2):
+        def project(i, half, passes=(0, 1), draining=False):
+            if passes[0] == 0:
+                projecting[i][half] = accumulator([P, BANK], draining)
+            acc = projecting[i][half]
+            for g in passes:
                 w_cols = slice(g * D + half * BANK, g * D + (half + 1) * BANK)
                 nc.tensor.matmul_mx(
                     out=acc[:],
@@ -391,30 +415,31 @@ def tile_sharedglobalattention_pb_kernel(tc, q_n, k_n, v, Wo, x, gate, log_tempe
                     start=(g == 0),
                     stop=(g == 1),
                 )
+
+        def add_residual(i, half):
             cols = slice(half * BANK, (half + 1) * BANK)
             result = projecting[i]["result"]
             nc.vector.scalar_tensor_tensor(
-                out=result[:, cols], in0=acc[:], scalar=gate_f[:, 0:1], in1=x_sb[:, i, cols], op0=ALU.mult, op1=ALU.add
+                out=result[:, cols], in0=projecting[i][half][:], scalar=gate_f[:, 0:1], in1=x_sb[:, i, cols],
+                op0=ALU.mult, op1=ALU.add,
             )
             nc.sync.dma_start(out=out[0, i * P : (i + 1) * P, cols], in_=result[:, cols])
 
-        n_items = len(items)
         other_run = {}
         needs = [(first_item[i], "q", i) for i in ORDER[2:]]
         for pair in range(2, Q_TILES, 2):
             needs.append((min(first_item[i] for i in range(pair, Q_TILES)), "k", pair))
         for need, kind, i in sorted(needs):
             slot = max(need - AHEAD, 0)
-            while slot in other_run and slot > 0:
+            while slot > 0 and (slot in other_run or (slot >= PROJECT_FIRST and slot % 2 == 1)):
                 slot = slot - 1
             while slot in other_run:
                 slot = slot + 1
             other_run[slot] = (kind, i)
-        multiply_slot = [min(j + LAG_V, max(n_items + 1, j + 2)) for j in range(n_items)]
         project_slot = {}
         earliest = PROJECT_FIRST
-        for i in ORDER:
-            slot = max(multiply_slot[last_item[i]] + 1, earliest)
+        for i in ORDER[:-2]:
+            slot = max(last_item[i] + LAG_V + 1, earliest)
             while slot in other_run:
                 slot = slot + 1
             other_run[slot] = ("a", i)
@@ -427,7 +452,7 @@ def tile_sharedglobalattention_pb_kernel(tc, q_n, k_n, v, Wo, x, gate, log_tempe
         scores_and_maxima(0, 0)
         scores_and_maxima(0, 1)
         transpose_q(ORDER[1])
-        for slot in range(0, max(project_slot) + 3):
+        for slot in range(0, n_items):
             if 0 <= slot - 2 < n_items:
                 quantise_e(slot - 2)
             if slot - 1 in project_slot:
@@ -444,14 +469,13 @@ def tile_sharedglobalattention_pb_kernel(tc, q_n, k_n, v, Wo, x, gate, log_tempe
                 {"q": transpose_q, "k": transpose_k, "a": transpose_a}[kind](i)
             if slot + 1 < n_items:
                 scores_and_maxima(slot + 1, 1)
-            for j in range(n_items):
-                if slot == multiply_slot[j]:
-                    multiply_v(j)
-                    normalise(j)
-            if slot - 1 in project_slot:
-                project(project_slot[slot - 1], 0)
-            if slot - 2 in project_slot:
-                project(project_slot[slot - 2], 1)
+            if slot >= LAG_V:
+                multiply_v(slot - LAG_V)
+                normalise(slot - LAG_V)
+            for half in range(2):
+                if slot - 1 - half in project_slot:
+                    project(project_slot[slot - 1 - half], half, draining=(slot == n_items - 1))
+                    add_residual(project_slot[slot - 1 - half], half)
             if 0 <= slot - WO_GPSIMD < 8:
                 w = 2 + (slot - WO_GPSIMD) // 4
                 regroup_wo(w, (slot - WO_GPSIMD) % 4, 4, regroup_on_gpsimd)
@@ -470,3 +494,31 @@ def tile_sharedglobalattention_pb_kernel(tc, q_n, k_n, v, Wo, x, gate, log_tempe
                 nc.vector.tensor_copy(out=gate_f[:], in_=gate_bf[:])
             if slot == V_SECOND_SLOT + 2:
                 quantise_v(1)
+
+        last = n_items - 1
+        before, final = ORDER[-2], ORDER[-1]
+        transpose_e(last, (0,), True)
+        transpose_e(last, (1,), True)
+        quantise_e(last - 1)
+        multiply_v(last - 2)
+        normalise(last - 2)
+        quantise_e(last, (0,))
+        quantise_e(last, (1,))
+        transpose_a(before)
+        multiply_v(last - 1)
+        normalise(last - 1)
+        multiply_v(last, True)
+        normalise(last)
+        quantise_a(before)
+        transpose_a(final, (0,))
+        quantise_a(final, (0,))
+        transpose_a(final, (1,), True)
+        quantise_a(final, (1,))
+        for half in range(2):
+            project(before, half)
+            add_residual(before, half)
+        for half in range(2):
+            project(final, half, (0,), True)
+        for half in range(2):
+            project(final, half, (1,), True)
+            add_residual(final, half)

@@ -24,15 +24,13 @@ K_PASS = 512
 BANK = 512
 HALF = 256
 MASKED = -1.0e30
-WO_GPSIMD = 3
-WO_VECTOR = 5
-WO_QUANT = [7, 9, 8, 12]
+WO_FIRST = 4
 PROJECT_FIRST = 11
 V_SECOND_SLOT = 3
 LAG_V = 3
 ORDER = [0, 1, 2, 3, 4, 5, 6, 7]
 PROJECT_STEP = 2
-AHEAD = 5
+AHEAD = 6
 LOADS = [(a[0], int(a[1])) for a in "q1 k2 v0 q2 q3 k4 q4 v1 g0 w0 q5 x0 k6 q6 x1 q7 x2 x3 x4 x5 x6 x7".split()]
 
 FLOPS = 2 * H * (512 * 512 + 512 * 1024) * HD * 2 + 2 * L * D * D
@@ -137,19 +135,11 @@ def tile_sharedglobalattention_pb_kernel(tc, q_n, k_n, v, Wo, x, gate, log_tempe
         nc.vector.tensor_copy(out=mask_bf[:], in_=mask_f32[:])
         scale = const.tile([P, 1], F32, name="scale")
         neg_scale = const.tile([P, 1], F32, name="neg_scale")
-        minus_one = const.tile([P, 2], F32, name="minus_one")
-        nc.gpsimd.memset(minus_one[:], -1.0)
         gate_f = const.tile([P, 1], F32, name="gate_f")
 
         def regroup(grouped, raw):
             nc.vector.tensor_copy(
                 out=grouped.rearrange("p (c i t) -> p c t i", i=4, t=4), in_=raw.rearrange("p t (c i) -> p c t i", i=4)
-            )
-
-        def regroup_on_gpsimd(grouped, raw):
-            nc.gpsimd.tensor_scalar(
-                out=grouped.rearrange("p (c i t) -> p c t i", i=4, t=4), in0=raw.rearrange("p t (c i) -> p c t i", i=4),
-                scalar1=1.0, scalar2=0.0, op0=ALU.mult, op1=ALU.add,
             )
 
         v_grouped = {}
@@ -249,8 +239,10 @@ def tile_sharedglobalattention_pb_kernel(tc, q_n, k_n, v, Wo, x, gate, log_tempe
                 nc.tensor.matmul(s[:, width - P : width], lhsT=ident_bf[:], rhs=mask_bf[:], start=False, stop=True)
             nc.vector.tensor_reduce(out=maxima[:, piece : piece + 1], in_=s[:, :width], axis=AXIS_X, op=ALU.max)
             live[j]["banks"].append((s, width))
-            if piece == 0:
-                return
+
+        def biases(j):
+            i, g, heads, chunks = items[j]
+            maxima = live[j]["maxima"]
             bias = small.tile([P, 2], F32, name="bias")
             if len(chunks) == 2:
                 nc.vector.tensor_scalar(
@@ -265,7 +257,10 @@ def tile_sharedglobalattention_pb_kernel(tc, q_n, k_n, v, Wo, x, gate, log_tempe
 
         def exponentials(j):
             i, g, heads, chunks = items[j]
-            row_sums = small.tile([P, 2], F32, name="row_sums")
+            if len(chunks) == 1 or heads[0] == 0:
+                row_sums = small.tile([P, PAIR, len(chunks)], F32, name="row_sums")
+            else:
+                row_sums = live[j - 1]["row_sums"]
             piece = 0
             for h in heads:
                 for c in chunks:
@@ -276,7 +271,7 @@ def tile_sharedglobalattention_pb_kernel(tc, q_n, k_n, v, Wo, x, gate, log_tempe
                         func=FUNC.Exp,
                         bias=live[j]["bias"][:, heads.index(h) : heads.index(h) + 1],
                         scale=scale[:, 0:1],
-                        accum_out=row_sums[:, piece : piece + 1],
+                        accum_out=row_sums[:, h, c : c + 1],
                     )
                     piece += 1
             live[j]["row_sums"] = row_sums
@@ -323,17 +318,22 @@ def tile_sharedglobalattention_pb_kernel(tc, q_n, k_n, v, Wo, x, gate, log_tempe
                 in_=words.bitcast(BF16),
             )
 
-        def invert_row_sums(j):
+        def add_row_sums(j):
             i, g, heads, chunks = items[j]
             row_sums = live[j]["row_sums"]
-            inverse = small.tile([P, 2], F32, name="inverse")
-            if len(chunks) == 2:
-                total = small.tile([P, 1], F32, name="total")
-                nc.gpsimd.tensor_tensor(out=total[:], in0=row_sums[:, 0:1], in1=row_sums[:, 1:2], op=ALU.add)
-                nc.gpsimd.tensor_tensor(out=inverse[:, 0:1], in0=total[:], in1=minus_one[:, 0:1], op=ALU.pow)
-            else:
-                nc.gpsimd.tensor_tensor(out=inverse[:], in0=row_sums[:], in1=minus_one[:], op=ALU.pow)
-            live[j]["inverse"] = inverse
+            if len(chunks) == 1:
+                live[j]["total"] = row_sums[:, :, 0]
+            elif heads[0] == 1:
+                total = small.tile([P, PAIR], F32, name="total")
+                nc.vector.tensor_tensor(out=total[:], in0=row_sums[:, :, 0], in1=row_sums[:, :, 1], op=ALU.add)
+                live[j]["total"] = total[:]
+
+        def invert_row_sums(j):
+            if "total" in live[j]:
+                inverse = small.tile([P, PAIR], F32, name="inverse")
+                nc.vector.reciprocal(out=inverse[:], in_=live[j]["total"])
+                for pair_item in (j,) if len(items[j][3]) == 1 else (j - 1, j):
+                    live[pair_item]["inverse"] = inverse
 
         def accumulator(shape, draining):
             if draining:
@@ -368,7 +368,7 @@ def tile_sharedglobalattention_pb_kernel(tc, q_n, k_n, v, Wo, x, gate, log_tempe
                     out=a_tiles[i][:, n * HD : (n + 1) * HD],
                     in_=o[:, heads.index(h), :],
                     func=FUNC.Copy,
-                    scale=inverse[:, heads.index(h) : heads.index(h) + 1],
+                    scale=inverse[:, h : h + 1],
                 )
 
         projecting = {}
@@ -431,7 +431,7 @@ def tile_sharedglobalattention_pb_kernel(tc, q_n, k_n, v, Wo, x, gate, log_tempe
             needs.append((min(first_item[i] for i in range(pair, Q_TILES)), "k", pair))
         for need, kind, i in sorted(needs):
             slot = max(need - AHEAD, 0)
-            while slot > 0 and (slot in other_run or (slot >= PROJECT_FIRST and slot % 2 == 1)):
+            while slot > 0 and (slot in other_run or (slot >= PROJECT_FIRST and slot % 2 == PROJECT_FIRST % 2)):
                 slot = slot - 1
             while slot in other_run:
                 slot = slot + 1
@@ -451,17 +451,19 @@ def tile_sharedglobalattention_pb_kernel(tc, q_n, k_n, v, Wo, x, gate, log_tempe
         nc.vector.tensor_scalar(out=neg_scale[:], in0=scale[:], scalar1=-1.0, scalar2=None, op0=ALU.mult)
         scores_and_maxima(0, 0)
         scores_and_maxima(0, 1)
+        biases(0)
         transpose_q(ORDER[1])
         for slot in range(0, n_items):
-            if 0 <= slot - 2 < n_items:
-                quantise_e(slot - 2)
+            if 0 <= slot - 1 < n_items:
+                add_row_sums(slot - 1)
             if slot - 1 in project_slot:
                 quantise_a(project_slot[slot - 1])
             if slot + 1 < n_items:
                 scores_and_maxima(slot + 1, 0)
+            if 0 <= slot - 1 < n_items:
+                invert_row_sums(slot - 1)
             if slot < n_items:
                 exponentials(slot)
-                invert_row_sums(slot)
             if 0 <= slot - 1 < n_items:
                 transpose_e(slot - 1)
             if slot in other_run:
@@ -469,6 +471,10 @@ def tile_sharedglobalattention_pb_kernel(tc, q_n, k_n, v, Wo, x, gate, log_tempe
                 {"q": transpose_q, "k": transpose_k, "a": transpose_a}[kind](i)
             if slot + 1 < n_items:
                 scores_and_maxima(slot + 1, 1)
+            if 0 <= slot - 2 < n_items:
+                quantise_e(slot - 2)
+            if slot + 1 < n_items:
+                biases(slot + 1)
             if slot >= LAG_V:
                 multiply_v(slot - LAG_V)
                 normalise(slot - LAG_V)
@@ -476,15 +482,11 @@ def tile_sharedglobalattention_pb_kernel(tc, q_n, k_n, v, Wo, x, gate, log_tempe
                 if slot - 1 - half in project_slot:
                     project(project_slot[slot - 1 - half], half, draining=(slot == n_items - 1))
                     add_residual(project_slot[slot - 1 - half], half)
-            if 0 <= slot - WO_GPSIMD < 8:
-                w = 2 + (slot - WO_GPSIMD) // 4
-                regroup_wo(w, (slot - WO_GPSIMD) % 4, 4, regroup_on_gpsimd)
-            if 0 <= slot - WO_VECTOR < 4:
-                w = (slot - WO_VECTOR) // 2
-                regroup_wo(w, (slot - WO_VECTOR) % 2, 2, regroup)
-            for w in range(4):
-                if slot == WO_QUANT[w]:
-                    quantise_wo(w)
+            quarters = [0, 2, 1, 3]
+            if 0 <= slot - WO_FIRST < 8:
+                regroup_wo(quarters[(slot - WO_FIRST) // 2], (slot - WO_FIRST) % 2, 2, regroup)
+            if 0 <= slot - WO_FIRST - 2 < 8 and (slot - WO_FIRST) % 2 == 0:
+                quantise_wo(quarters[(slot - WO_FIRST - 2) // 2])
             if slot == 0:
                 regroup_v(0)
             if slot == 2:
@@ -502,8 +504,10 @@ def tile_sharedglobalattention_pb_kernel(tc, q_n, k_n, v, Wo, x, gate, log_tempe
         quantise_e(last - 1)
         multiply_v(last - 2)
         normalise(last - 2)
+        add_row_sums(last)
         quantise_e(last, (0,))
         quantise_e(last, (1,))
+        invert_row_sums(last)
         transpose_a(before)
         multiply_v(last - 1)
         normalise(last - 1)

@@ -31,7 +31,7 @@ LAG_V = 3
 ORDER = [0, 1, 2, 3, 4, 5, 6, 7]
 PROJECT_STEP = 2
 AHEAD = 6
-LOADS = [(a[0], int(a[1])) for a in "q1 k2 v0 q2 q3 k4 q4 v1 g0 w0 q5 x0 k6 q6 x1 q7 x2 x3 x4 x5 x6 x7".split()]
+LOADS = [(a[0], int(a[1])) for a in "k2 v0 q2 k4 q4 v1 g0 w0 x0 k6 q6 x1 x2 x3 x4 x5 x6 x7".split()]
 
 FLOPS = 2 * H * (512 * 512 + 512 * 1024) * HD * 2 + 2 * L * D * D
 
@@ -48,12 +48,12 @@ def tile_sharedglobalattention_pb_kernel(tc, q_n, k_n, v, Wo, x, gate, log_tempe
         psum_t = ctx.enter_context(tc.psum_pool(name="psum_t", bufs=2))
         psum_acc = ctx.enter_context(tc.psum_pool(name="psum_acc", bufs=2))
 
-        q_raw = resident.tile([P, Q_TILES, H, HD], BF16, name="q_raw")
+        q_raw = resident.tile([P, H, Q_TILES, HD], BF16, name="q_raw")
         k_raw = resident.tile([P, KV, Q_TILES, HD], BF16, name="k_raw")
         v_raw = resident.tile([P, KV * L * HD // P], BF16, name="v_raw")
         wo_raw = resident.tile([P, D * D // P], BF16, name="wo_raw")
         x_sb = resident.tile([P, Q_TILES, D], BF16, name="x_sb")
-        q_t = resident.tile([P, Q_TILES, H, P], F32, name="q_t")
+        q_t = resident.tile([P, H, L], F32, name="q_t")
         k_t = resident.tile([P, KV, L], F32, name="k_t")
         v_codes = resident.tile([P, KV * 2 * HD], U32, name="v_codes", align_bytes=64)
         v_scales = resident.tile([P, KV * 2 * HD], U8, name="v_scales", align_bytes=64)
@@ -68,16 +68,24 @@ def tile_sharedglobalattention_pb_kernel(tc, q_n, k_n, v, Wo, x, gate, log_tempe
         lt_bf = const.tile([P, 1], BF16, name="lt_bf")
         gate_bf = const.tile([P, 1], BF16, name="gate_bf")
 
-        def load_k(i, groups=range(KV)):
-            for g in groups:
+        def load_k(i):
+            for g in range(KV):
                 nc.sync.dma_start(
                     out=k_raw[:, g, i : i + 2, :],
-                    in_=k_n[0, g, i * P : (i + 2) * P, :].rearrange("(t p) d -> p t d", p=P),
+                    in_=k_n[0, g, i * P : (i + 2) * P, :].rearrange("(p t) d -> p t d", t=2),
                 )
 
-        def load_q(i, heads=slice(0, H)):
+        def load_q(i):
+            for g in range(KV):
+                heads = slice(g * PAIR, (g + 1) * PAIR)
+                nc.sync.dma_start(
+                    out=q_raw[:, heads, i : i + 2, :],
+                    in_=q_n[0, heads, i * P : (i + 2) * P, :].rearrange("n (p t) d -> p n t d", t=2),
+                )
+
+        def load_q_tile(i, heads):
             nc.sync.dma_start(
-                out=q_raw[:, i, heads, :], in_=q_n[0, heads, i * P : (i + 1) * P, :].rearrange("n p d -> p n d")
+                out=q_raw[:, heads, i, :], in_=q_n[0, heads, i * P : (i + 1) * P, :].rearrange("n p d -> p n d")
             )
 
         def load_v(c):
@@ -99,12 +107,15 @@ def tile_sharedglobalattention_pb_kernel(tc, q_n, k_n, v, Wo, x, gate, log_tempe
             nc.sync.dma_start(out=x_sb[:, i, :], in_=x[0, i * P : (i + 1) * P, :])
 
         for g in range(KV):
-            load_k(0, [g])
-            load_q(ORDER[0], slice(g * PAIR, (g + 1) * PAIR))
+            nc.sync.dma_start(
+                out=k_raw[:, g, 0:2, :], in_=k_n[0, g, 0 : 2 * P, :].rearrange("(t p) d -> p t d", p=P)
+            )
+            load_q_tile(0, slice(g * PAIR, (g + 1) * PAIR))
         nc.sync.dma_start(out=lt_bf[:], in_=log_temperature.partition_broadcast(P))
         def load_gate(i):
             nc.sync.dma_start(out=gate_bf[:], in_=gate.partition_broadcast(P))
 
+        load_q_tile(1, slice(0, H))
         for name, arg in LOADS:
             {"q": load_q, "k": load_k, "v": load_v, "x": load_x, "w": load_wo, "g": load_gate}[name](arg)
 
@@ -183,23 +194,36 @@ def tile_sharedglobalattention_pb_kernel(tc, q_n, k_n, v, Wo, x, gate, log_tempe
             nc.scalar.copy(out=k_t[:, g, : 2 * P].rearrange("p (t k) -> p t k", t=2), in_=bank[:])
             bank = pool.tile([P, PAIR, P], F32, name="bank_q0", tag=tag)
             for h in range(PAIR):
-                nc.tensor.transpose(bank[:, h, :], q_raw[:, ORDER[0], g * PAIR + h, :].bitcast(F32), ident_f32[:])
-            nc.vector.tensor_copy(out=q_t[:, ORDER[0], g * PAIR : (g + 1) * PAIR, :], in_=bank[:])
+                nc.tensor.transpose(bank[:, h, :], q_raw[:, g * PAIR + h, 0, :].bitcast(F32), ident_f32[:])
+            nc.vector.tensor_copy(out=q_t[:, g * PAIR : (g + 1) * PAIR, :P], in_=bank[:])
 
-        def transpose_q(i):
-            bank = psum_t.tile([P, H, P], F32, name="bank_q", tag="t")
+        def transpose_second():
+            bank = psum_t.tile([P, H, P], F32, name="bank_q1", tag="t")
             for n in range(H):
-                nc.tensor.transpose(bank[:, n, :], q_raw[:, i, n, :].bitcast(F32), ident_f32[:])
-            nc.scalar.copy(out=q_t[:, i, :, :], in_=bank[:])
+                nc.tensor.transpose(bank[:, n, :], q_raw[:, n, 1, :].bitcast(F32), ident_f32[:])
+            nc.scalar.copy(out=q_t[:, :, P : 2 * P], in_=bank[:])
+
+        def transpose_q(i, g):
+            bank = psum_t.tile([P, PAIR, 2, P], F32, name="bank_q", tag="t")
+            heads = slice(g * PAIR, (g + 1) * PAIR)
+            pairs = []
+            for h in range(PAIR):
+                for t in range(2):
+                    pairs.append((bank[:, h, t, :], q_raw[:, g * PAIR + h, i + t, :].bitcast(F32)))
+            return pairs, lambda: nc.scalar.copy(
+                out=q_t[:, heads, i * P : (i + 2) * P].rearrange("p h (k t) -> p h k t", t=2),
+                in_=bank[:].rearrange("p h t k -> p h k t"),
+            )
 
         def transpose_k(i):
             bank = psum_t.tile([P, KV, 2, P], F32, name="bank_k", tag="t")
+            pairs = []
             for g in range(KV):
                 for t in range(2):
-                    nc.tensor.transpose(bank[:, g, t, :], k_raw[:, g, i + t, :].bitcast(F32), ident_f32[:])
-            nc.scalar.copy(
-                out=k_t[:, :, i * P : (i + 2) * P].rearrange("p g (t k) -> p g t k", t=2),
-                in_=bank[:],
+                    pairs.append((bank[:, g, t, :], k_raw[:, g, i + t, :].bitcast(F32)))
+            return pairs, lambda: nc.scalar.copy(
+                out=k_t[:, :, i * P : (i + 2) * P].rearrange("p g (k t) -> p g k t", t=2),
+                in_=bank[:].rearrange("p g t k -> p g k t"),
             )
 
         items = []
@@ -217,7 +241,7 @@ def tile_sharedglobalattention_pb_kernel(tc, q_n, k_n, v, Wo, x, gate, log_tempe
         n_items = len(items)
         live = {}
 
-        def scores_and_maxima(j, piece):
+        def scores_and_maxima(j, piece, between):
             i, g, heads, chunks = items[j]
             keys = (i + 1) * P
             h, c = [(h, c) for h in heads for c in chunks][piece]
@@ -230,11 +254,12 @@ def tile_sharedglobalattention_pb_kernel(tc, q_n, k_n, v, Wo, x, gate, log_tempe
             for e in range(2):
                 nc.tensor.matmul(
                     s[:, :width],
-                    lhsT=halves(q_t[:, i, g * PAIR + h, :])[:, :, e],
+                    lhsT=halves(q_t[:, g * PAIR + h, i * P : (i + 1) * P])[:, :, e],
                     rhs=halves(k_t[:, g, c * K_PASS : c * K_PASS + width])[:, :, e],
                     start=(e == 0),
                     stop=(e == 1 and not diagonal),
                 )
+                between()
             if diagonal:
                 nc.tensor.matmul(s[:, width - P : width], lhsT=ident_bf[:], rhs=mask_bf[:], start=False, stop=True)
             nc.vector.tensor_reduce(out=maxima[:, piece : piece + 1], in_=s[:, :width], axis=AXIS_X, op=ALU.max)
@@ -292,19 +317,17 @@ def tile_sharedglobalattention_pb_kernel(tc, q_n, k_n, v, Wo, x, gate, log_tempe
             i, g, heads, chunks = items[j]
             n_pieces = len(pieces)
             bank = transpose_bank(n_pieces, draining)
+            pairs = []
             for piece in pieces:
                 h, c = [(h, c) for h in heads for c in chunks][piece]
                 for u in range(2):
                     first_key = c * K_PASS + u * HALF
-                    nc.tensor.transpose(
-                        bank[:, piece - pieces[0], u, :],
-                        e_tiles[i][:, g * PAIR + h, first_key : first_key + HALF].bitcast(F32),
-                        ident_f32[:],
-                    )
+                    keys = e_tiles[i][:, g * PAIR + h, first_key : first_key + HALF]
+                    pairs.append((bank[:, piece - pieces[0], u, :], keys.bitcast(F32)))
             if pieces[0] == 0:
                 live[j]["e_grouped"] = work.tile([P, 2 * P * 2], F32, name="e_grouped", align_bytes=64)
             words = live[j]["e_grouped"][:, pieces[0] * P * 2 : (pieces[-1] + 1) * P * 2]
-            copy_out(words, bank, n_pieces, j == n_items - 2)
+            return pairs, lambda: copy_out(words, bank, n_pieces, j == n_items - 2)
 
         def quantise_e(j, pieces=(0, 1)):
             if pieces[0] == 0:
@@ -376,16 +399,15 @@ def tile_sharedglobalattention_pb_kernel(tc, q_n, k_n, v, Wo, x, gate, log_tempe
         def transpose_a(i, passes=(0, 1), draining=False):
             n_passes = len(passes)
             bank = transpose_bank(n_passes, draining)
+            pairs = []
             for g in passes:
                 for u in range(2):
                     first = g * K_PASS + u * HALF
-                    nc.tensor.transpose(
-                        bank[:, g - passes[0], u, :], a_tiles[i][:, first : first + HALF].bitcast(F32), ident_f32[:]
-                    )
+                    pairs.append((bank[:, g - passes[0], u, :], a_tiles[i][:, first : first + HALF].bitcast(F32)))
             if passes[0] == 0:
                 projecting[i] = {"a_grouped": work.tile([P, 2 * P * 2], F32, name="a_grouped", align_bytes=64)}
             words = projecting[i]["a_grouped"][:, passes[0] * P * 2 : (passes[-1] + 1) * P * 2]
-            copy_out(words, bank, n_passes, i == ORDER[-2])
+            return pairs, lambda: copy_out(words, bank, n_passes, i == ORDER[-2])
 
         def quantise_a(i, passes=(0, 1)):
             if passes[0] == 0:
@@ -416,26 +438,31 @@ def tile_sharedglobalattention_pb_kernel(tc, q_n, k_n, v, Wo, x, gate, log_tempe
                     stop=(g == 1),
                 )
 
-        def add_residual(i, half):
-            cols = slice(half * BANK, (half + 1) * BANK)
+        def add_residual(i, half, parts=1):
             result = projecting[i]["result"]
-            nc.vector.scalar_tensor_tensor(
-                out=result[:, cols], in0=projecting[i][half][:], scalar=gate_f[:, 0:1], in1=x_sb[:, i, cols],
-                op0=ALU.mult, op1=ALU.add,
-            )
-            nc.sync.dma_start(out=out[0, i * P : (i + 1) * P, cols], in_=result[:, cols])
+            width = BANK // parts
+            for part in range(parts):
+                bank_cols = slice(part * width, (part + 1) * width)
+                cols = slice(half * BANK + part * width, half * BANK + (part + 1) * width)
+                nc.vector.scalar_tensor_tensor(
+                    out=result[:, cols], in0=projecting[i][half][:, bank_cols], scalar=gate_f[:, 0:1],
+                    in1=x_sb[:, i, cols], op0=ALU.mult, op1=ALU.add,
+                )
+                nc.sync.dma_start(out=out[0, i * P : (i + 1) * P, cols], in_=result[:, cols])
 
         other_run = {}
-        needs = [(first_item[i], "q", i) for i in ORDER[2:]]
-        for pair in range(2, Q_TILES, 2):
-            needs.append((min(first_item[i] for i in range(pair, Q_TILES)), "k", pair))
-        for need, kind, i in sorted(needs):
+        needs = []
+        for i in range(2, Q_TILES, 2):
+            needs.append((first_item[i], ("k", i)))
+            for g in range(KV):
+                needs.append((first_item[i] + g * (1 if i < 4 else 2), ("q", i, g)))
+        for need, run in sorted(needs):
             slot = max(need - AHEAD, 0)
             while slot > 0 and (slot in other_run or (slot >= PROJECT_FIRST and slot % 2 == PROJECT_FIRST % 2)):
                 slot = slot - 1
             while slot in other_run:
                 slot = slot + 1
-            other_run[slot] = (kind, i)
+            other_run[slot] = run
         project_slot = {}
         earliest = PROJECT_FIRST
         for i in ORDER[:-2]:
@@ -449,28 +476,51 @@ def tile_sharedglobalattention_pb_kernel(tc, q_n, k_n, v, Wo, x, gate, log_tempe
         transpose_first(1)
         nc.scalar.activation(out=scale[:], in_=lt_bf[:], func=FUNC.Exp)
         nc.vector.tensor_scalar(out=neg_scale[:], in0=scale[:], scalar1=-1.0, scalar2=None, op0=ALU.mult)
-        scores_and_maxima(0, 0)
-        scores_and_maxima(0, 1)
+        def weave(pairs, gaps):
+            calls = []
+
+            def between():
+                n = len(calls)
+                calls.append(n)
+                if n < gaps:
+                    for out_words, in_words in pairs[len(pairs) * n // gaps : len(pairs) * (n + 1) // gaps]:
+                        nc.tensor.transpose(out_words, in_words, ident_f32[:])
+
+            return between
+
+        def transpose_now(run):
+            pairs, copy = run
+            weave(pairs, 1)()
+            copy()
+
+        scores_and_maxima(0, 0, weave([], 1))
+        scores_and_maxima(0, 1, weave([], 1))
         biases(0)
-        transpose_q(ORDER[1])
+        transpose_second()
         for slot in range(0, n_items):
             if 0 <= slot - 1 < n_items:
                 add_row_sums(slot - 1)
             if slot - 1 in project_slot:
                 quantise_a(project_slot[slot - 1])
-            if slot + 1 < n_items:
-                scores_and_maxima(slot + 1, 0)
-            if 0 <= slot - 1 < n_items:
-                invert_row_sums(slot - 1)
-            if slot < n_items:
-                exponentials(slot)
-            if 0 <= slot - 1 < n_items:
-                transpose_e(slot - 1)
+            exponentials(slot)
+            runs = []
+            if slot >= 1:
+                runs.append(transpose_e(slot - 1))
             if slot in other_run:
-                kind, i = other_run[slot]
-                {"q": transpose_q, "k": transpose_k, "a": transpose_a}[kind](i)
+                run = other_run[slot]
+                runs.append({"q": transpose_q, "k": transpose_k, "a": transpose_a}[run[0]](*run[1:]))
+            pairs = [pair for run in runs for pair in run[0]]
             if slot + 1 < n_items:
-                scores_and_maxima(slot + 1, 1)
+                between = weave(pairs, 4)
+                scores_and_maxima(slot + 1, 0, between)
+                if slot >= 1:
+                    invert_row_sums(slot - 1)
+                scores_and_maxima(slot + 1, 1, between)
+            else:
+                invert_row_sums(slot - 1)
+                weave(pairs, 1)()
+            for run in runs:
+                run[1]()
             if 0 <= slot - 2 < n_items:
                 quantise_e(slot - 2)
             if slot + 1 < n_items:
@@ -499,8 +549,8 @@ def tile_sharedglobalattention_pb_kernel(tc, q_n, k_n, v, Wo, x, gate, log_tempe
 
         last = n_items - 1
         before, final = ORDER[-2], ORDER[-1]
-        transpose_e(last, (0,), True)
-        transpose_e(last, (1,), True)
+        transpose_now(transpose_e(last, (0,), True))
+        transpose_now(transpose_e(last, (1,), True))
         quantise_e(last - 1)
         multiply_v(last - 2)
         normalise(last - 2)
@@ -508,15 +558,15 @@ def tile_sharedglobalattention_pb_kernel(tc, q_n, k_n, v, Wo, x, gate, log_tempe
         quantise_e(last, (0,))
         quantise_e(last, (1,))
         invert_row_sums(last)
-        transpose_a(before)
+        transpose_now(transpose_a(before))
         multiply_v(last - 1)
         normalise(last - 1)
         multiply_v(last, True)
         normalise(last)
         quantise_a(before)
-        transpose_a(final, (0,))
+        transpose_now(transpose_a(final, (0,)))
         quantise_a(final, (0,))
-        transpose_a(final, (1,), True)
+        transpose_now(transpose_a(final, (1,), True))
         quantise_a(final, (1,))
         for half in range(2):
             project(before, half)
@@ -525,4 +575,4 @@ def tile_sharedglobalattention_pb_kernel(tc, q_n, k_n, v, Wo, x, gate, log_tempe
             project(final, half, (0,), True)
         for half in range(2):
             project(final, half, (1,), True)
-            add_residual(final, half)
+            add_residual(final, half, 1 + half)

@@ -48,13 +48,15 @@ def tile_sharedglobalattention_pb_kernel(tc, q_n, k_n, v, Wo, x, gate, log_tempe
         psum_t = ctx.enter_context(tc.psum_pool(name="psum_t", bufs=2))
         psum_acc = ctx.enter_context(tc.psum_pool(name="psum_acc", bufs=2))
 
-        q_raw = resident.tile([P, H, Q_TILES, HD], BF16, name="q_raw")
+        q_raw_first = resident.tile([P, 2, H, HD], BF16, name="q_raw_first")
+        q_raw = resident.tile([P, Q_TILES // 2 - 1, KV, PAIR, 2, HD], BF16, name="q_raw")
         k_raw = resident.tile([P, KV, Q_TILES, HD], BF16, name="k_raw")
         v_raw = resident.tile([P, KV * L * HD // P], BF16, name="v_raw")
         wo_raw = resident.tile([P, D * D // P], BF16, name="wo_raw")
         x_sb = resident.tile([P, Q_TILES, D], BF16, name="x_sb")
-        q_t = resident.tile([P, H, L], F32, name="q_t")
-        k_t = resident.tile([P, KV, L], F32, name="k_t")
+        q_t_first = resident.tile([P, 2, H, P], F32, name="q_t_first")
+        q_t = resident.tile([P, Q_TILES // 2 - 1, KV, PAIR, 2 * P], F32, name="q_t")
+        k_t = [resident.tile([P, L], F32, name="k_t%d" % g) for g in range(KV)]
         v_codes = resident.tile([P, KV * 2 * HD], U32, name="v_codes", align_bytes=64)
         v_scales = resident.tile([P, KV * 2 * HD], U8, name="v_scales", align_bytes=64)
         wo_codes = resident.tile([P, 2 * D], U32, name="wo_codes", align_bytes=64)
@@ -79,13 +81,13 @@ def tile_sharedglobalattention_pb_kernel(tc, q_n, k_n, v, Wo, x, gate, log_tempe
             for g in range(KV):
                 heads = slice(g * PAIR, (g + 1) * PAIR)
                 nc.sync.dma_start(
-                    out=q_raw[:, heads, i : i + 2, :],
+                    out=q_raw[:, i // 2 - 1, g, :, :, :],
                     in_=q_n[0, heads, i * P : (i + 2) * P, :].rearrange("n (p t) d -> p n t d", t=2),
                 )
 
         def load_q_tile(i, heads):
             nc.sync.dma_start(
-                out=q_raw[:, heads, i, :], in_=q_n[0, heads, i * P : (i + 1) * P, :].rearrange("n p d -> p n d")
+                out=q_raw_first[:, i, heads, :], in_=q_n[0, heads, i * P : (i + 1) * P, :].rearrange("n p d -> p n d")
             )
 
         def load_v(c):
@@ -191,27 +193,26 @@ def tile_sharedglobalattention_pb_kernel(tc, q_n, k_n, v, Wo, x, gate, log_tempe
             bank = pool.tile([P, 2, P], F32, name="bank_k0", tag=tag)
             for t in range(2):
                 nc.tensor.transpose(bank[:, t, :], k_raw[:, g, t, :].bitcast(F32), ident_f32[:])
-            nc.scalar.copy(out=k_t[:, g, : 2 * P].rearrange("p (t k) -> p t k", t=2), in_=bank[:])
+            nc.scalar.copy(out=k_t[g][:, : 2 * P].rearrange("p (t k) -> p t k", t=2), in_=bank[:])
             bank = pool.tile([P, PAIR, P], F32, name="bank_q0", tag=tag)
             for h in range(PAIR):
-                nc.tensor.transpose(bank[:, h, :], q_raw[:, g * PAIR + h, 0, :].bitcast(F32), ident_f32[:])
-            nc.vector.tensor_copy(out=q_t[:, g * PAIR : (g + 1) * PAIR, :P], in_=bank[:])
+                nc.tensor.transpose(bank[:, h, :], q_raw_first[:, 0, g * PAIR + h, :].bitcast(F32), ident_f32[:])
+            nc.vector.tensor_copy(out=q_t_first[:, 0, g * PAIR : (g + 1) * PAIR, :], in_=bank[:])
 
         def transpose_second():
             bank = psum_t.tile([P, H, P], F32, name="bank_q1", tag="t")
             for n in range(H):
-                nc.tensor.transpose(bank[:, n, :], q_raw[:, n, 1, :].bitcast(F32), ident_f32[:])
-            nc.scalar.copy(out=q_t[:, :, P : 2 * P], in_=bank[:])
+                nc.tensor.transpose(bank[:, n, :], q_raw_first[:, 1, n, :].bitcast(F32), ident_f32[:])
+            nc.scalar.copy(out=q_t_first[:, 1, :, :], in_=bank[:])
 
         def transpose_q(i, g):
             bank = psum_t.tile([P, PAIR, 2, P], F32, name="bank_q", tag="t")
-            heads = slice(g * PAIR, (g + 1) * PAIR)
             pairs = []
             for h in range(PAIR):
                 for t in range(2):
-                    pairs.append((bank[:, h, t, :], q_raw[:, g * PAIR + h, i + t, :].bitcast(F32)))
+                    pairs.append((bank[:, h, t, :], q_raw[:, i // 2 - 1, g, h, t, :].bitcast(F32)))
             return pairs, lambda: nc.scalar.copy(
-                out=q_t[:, heads, i * P : (i + 2) * P].rearrange("p h (k t) -> p h k t", t=2),
+                out=q_t[:, i // 2 - 1, g, :, :].rearrange("p h (k t) -> p h k t", t=2),
                 in_=bank[:].rearrange("p h t k -> p h k t"),
             )
 
@@ -221,10 +222,15 @@ def tile_sharedglobalattention_pb_kernel(tc, q_n, k_n, v, Wo, x, gate, log_tempe
             for g in range(KV):
                 for t in range(2):
                     pairs.append((bank[:, g, t, :], k_raw[:, g, i + t, :].bitcast(F32)))
-            return pairs, lambda: nc.scalar.copy(
-                out=k_t[:, :, i * P : (i + 2) * P].rearrange("p g (k t) -> p g k t", t=2),
-                in_=bank[:].rearrange("p g t k -> p g k t"),
-            )
+
+            def copy():
+                for g in range(KV):
+                    nc.scalar.copy(
+                        out=k_t[g][:, i * P : (i + 2) * P].rearrange("p (k t) -> p k t", t=2),
+                        in_=bank[:, g, :, :].rearrange("p t k -> p k t"),
+                    )
+
+            return pairs, copy
 
         items = []
         first_item = [0] * Q_TILES
@@ -251,11 +257,15 @@ def tile_sharedglobalattention_pb_kernel(tc, q_n, k_n, v, Wo, x, gate, log_tempe
             width = min(K_PASS, keys - c * K_PASS)
             s = psum_s.tile([P, BANK], F32, name="s")
             diagonal = c == chunks[-1]
+            if i < 2:
+                queries = q_t_first[:, i, g * PAIR + h, :]
+            else:
+                queries = q_t[:, i // 2 - 1, g, h, i % 2 * P : (i % 2 + 1) * P]
             for e in range(2):
                 nc.tensor.matmul(
                     s[:, :width],
-                    lhsT=halves(q_t[:, g * PAIR + h, i * P : (i + 1) * P])[:, :, e],
-                    rhs=halves(k_t[:, g, c * K_PASS : c * K_PASS + width])[:, :, e],
+                    lhsT=halves(queries)[:, :, e],
+                    rhs=halves(k_t[g][:, c * K_PASS : c * K_PASS + width])[:, :, e],
                     start=(e == 0),
                     stop=(e == 1 and not diagonal),
                 )

@@ -26,12 +26,13 @@ HALF = 256
 MASKED = -1.0e30
 WO_FIRST = 4
 PROJECT_FIRST = 11
-V_SECOND_SLOT = 3
+V_REGROUP = [0, 3]
+SCALAR_STEP = 16
 LAG_V = 3
 ORDER = [0, 1, 2, 3, 4, 5, 6, 7]
 PROJECT_STEP = 2
 AHEAD = 6
-LOADS = [(a[0], int(a[1])) for a in "k2 v0 q2 k4 q4 v1 g0 w0 x0 k6 q6 x1 x2 x3 x4 x5 x6 x7".split()]
+LOADS = [(a[0], int(a[1])) for a in "k2 v0 q2 k4 q4 v1 w0 x0 k6 q6 x1 x2 x3 x4 x5 x6 x7".split()]
 
 FLOPS = 2 * H * (512 * 512 + 512 * 1024) * HD * 2 + 2 * L * D * D
 
@@ -67,8 +68,8 @@ def tile_sharedglobalattention_pb_kernel(tc, q_n, k_n, v, Wo, x, gate, log_tempe
             e_tiles.append(resident.tile([P, H, K_PASS * (i // 4 + 1)], BF16, name="e%d" % i))
             a_tiles.append(resident.tile([P, D], BF16, name="a%d" % i))
 
-        lt_bf = const.tile([P, 1], BF16, name="lt_bf")
-        gate_bf = const.tile([P, 1], BF16, name="gate_bf")
+        scalars = const.tile([P, 2 * SCALAR_STEP], BF16, name="scalars")
+        nc.vector.memset(scalars[:], 0.0)
 
         def load_k(i):
             for g in range(KV):
@@ -113,13 +114,11 @@ def tile_sharedglobalattention_pb_kernel(tc, q_n, k_n, v, Wo, x, gate, log_tempe
                 out=k_raw[:, g, 0:2, :], in_=k_n[0, g, 0 : 2 * P, :].rearrange("(t p) d -> p t d", p=P)
             )
             load_q_tile(0, slice(g * PAIR, (g + 1) * PAIR))
-        nc.sync.dma_start(out=lt_bf[:], in_=log_temperature.partition_broadcast(P))
-        def load_gate(i):
-            nc.sync.dma_start(out=gate_bf[:], in_=gate.partition_broadcast(P))
-
+        nc.sync.dma_start(out=scalars[0:1, 0:1], in_=log_temperature.unsqueeze(0))
+        nc.sync.dma_start(out=scalars[0:1, SCALAR_STEP : SCALAR_STEP + 1], in_=gate.unsqueeze(0))
         load_q_tile(1, slice(0, H))
         for name, arg in LOADS:
-            {"q": load_q, "k": load_k, "v": load_v, "x": load_x, "w": load_wo, "g": load_gate}[name](arg)
+            {"q": load_q, "k": load_k, "v": load_v, "x": load_x, "w": load_wo}[name](arg)
 
         warm = const.tile([P, 1], F32, name="warm")
         nc.vector.memset(warm[:], 0.0)
@@ -146,6 +145,8 @@ def tile_sharedglobalattention_pb_kernel(tc, q_n, k_n, v, Wo, x, gate, log_tempe
         )
         mask_bf = const.tile([P, P], BF16, name="mask_bf")
         nc.vector.tensor_copy(out=mask_bf[:], in_=mask_f32[:])
+        ones_bf = const.tile([P, P], BF16, name="ones_bf")
+        nc.vector.memset(ones_bf[:], 1.0)
         scale = const.tile([P, 1], F32, name="scale")
         neg_scale = const.tile([P, 1], F32, name="neg_scale")
         gate_f = const.tile([P, 1], F32, name="gate_f")
@@ -157,11 +158,10 @@ def tile_sharedglobalattention_pb_kernel(tc, q_n, k_n, v, Wo, x, gate, log_tempe
 
         v_grouped = {}
 
-        def regroup_v(c):
-            for g in range(KV):
-                cols = slice((g * 2 + c) * 4 * HD, (g * 2 + c + 1) * 4 * HD)
-                v_grouped[g] = work.tile([P, 4 * HD], BF16, name="v_grouped", align_bytes=64)
-                regroup(v_grouped[g][:], v_raw[:, cols].rearrange("p (t d) -> p t d", t=4))
+        def regroup_v(g, c):
+            cols = slice((g * 2 + c) * 4 * HD, (g * 2 + c + 1) * 4 * HD)
+            v_grouped[g] = work.tile([P, 4 * HD], BF16, name="v_grouped", align_bytes=64)
+            regroup(v_grouped[g][:], v_raw[:, cols].rearrange("p (t d) -> p t d", t=4))
 
         def quantise_v(c):
             for g in range(KV):
@@ -484,7 +484,10 @@ def tile_sharedglobalattention_pb_kernel(tc, q_n, k_n, v, Wo, x, gate, log_tempe
             earliest = slot + PROJECT_STEP
         transpose_first(0)
         transpose_first(1)
-        nc.scalar.activation(out=scale[:], in_=lt_bf[:], func=FUNC.Exp)
+        spread = psum_s.tile([P, 2 * SCALAR_STEP], F32, name="spread", tag="s")
+        nc.tensor.matmul(spread[:], lhsT=ones_bf[:], rhs=scalars[:], start=True, stop=True)
+        nc.scalar.activation(out=scale[:], in_=spread[:, 0:1], func=FUNC.Exp)
+        nc.vector.tensor_copy(out=gate_f[:], in_=spread[:, SCALAR_STEP : SCALAR_STEP + 1])
         nc.vector.tensor_scalar(out=neg_scale[:], in0=scale[:], scalar1=-1.0, scalar2=None, op0=ALU.mult)
         def weave(pairs, gaps):
             calls = []
@@ -538,24 +541,22 @@ def tile_sharedglobalattention_pb_kernel(tc, q_n, k_n, v, Wo, x, gate, log_tempe
             if slot >= LAG_V:
                 multiply_v(slot - LAG_V)
                 normalise(slot - LAG_V)
-            for half in range(2):
-                if slot - 1 - half in project_slot:
-                    project(project_slot[slot - 1 - half], half, draining=(slot == n_items - 1))
-                    add_residual(project_slot[slot - 1 - half], half)
+            for g in range(KV):
+                for c in range(2):
+                    if slot == V_REGROUP[c] + g:
+                        regroup_v(g, c)
+            for c in range(2):
+                if slot == V_REGROUP[c] + 2:
+                    quantise_v(c)
             quarters = [0, 2, 1, 3]
             if 0 <= slot - WO_FIRST < 8:
                 regroup_wo(quarters[(slot - WO_FIRST) // 2], (slot - WO_FIRST) % 2, 2, regroup)
             if 0 <= slot - WO_FIRST - 2 < 8 and (slot - WO_FIRST) % 2 == 0:
                 quantise_wo(quarters[(slot - WO_FIRST - 2) // 2])
-            if slot == 0:
-                regroup_v(0)
-            if slot == 2:
-                quantise_v(0)
-            if slot == V_SECOND_SLOT:
-                regroup_v(1)
-                nc.vector.tensor_copy(out=gate_f[:], in_=gate_bf[:])
-            if slot == V_SECOND_SLOT + 2:
-                quantise_v(1)
+            for half in range(2):
+                if slot - 1 - half in project_slot:
+                    project(project_slot[slot - 1 - half], half, draining=(slot == n_items - 1))
+                    add_residual(project_slot[slot - 1 - half], half)
 
         last = n_items - 1
         before, final = ORDER[-2], ORDER[-1]

@@ -27,6 +27,7 @@ MASKED = -1.0e30
 WO_FIRST = 4
 PROJECT_FIRST = 11
 V_REGROUP = [0, 3]
+WARM_UP = 4
 SCALAR_STEP = 16
 LAG_V = 3
 ORDER = [0, 1, 2, 3, 4, 5, 6, 7]
@@ -120,6 +121,8 @@ def tile_sharedglobalattention_pb_kernel(tc, q_n, k_n, v, Wo, x, gate, log_tempe
         for name, arg in LOADS:
             {"q": load_q, "k": load_k, "v": load_v, "x": load_x, "w": load_wo}[name](arg)
 
+        zeros = const.tile([P, BANK], BF16, name="zeros")
+        nc.vector.memset(zeros[:].bitcast(F32), 0.0)
         warm = const.tile([P, 1], F32, name="warm")
         nc.vector.memset(warm[:], 0.0)
         nc.scalar.activation(out=warm[:], in_=warm[:], func=FUNC.Exp)
@@ -482,6 +485,9 @@ def tile_sharedglobalattention_pb_kernel(tc, q_n, k_n, v, Wo, x, gate, log_tempe
             other_run[slot] = ("a", i)
             project_slot[slot] = i
             earliest = slot + PROJECT_STEP
+        dummy = psum_s.tile([P, BANK], F32, name="dummy", tag="s")
+        for n in range(WARM_UP):
+            nc.tensor.matmul(dummy[:], lhsT=zeros[:, :P], rhs=zeros[:], start=True, stop=True)
         transpose_first(0)
         transpose_first(1)
         spread = psum_s.tile([P, 2 * SCALAR_STEP], F32, name="spread", tag="s")

@@ -530,8 +530,8 @@ def tile_sharedglobalattention_pb_kernel(tc, q_n, k_n, v, Wo, x, gate, log_tempe
                 runs.append({"q": transpose_q, "k": transpose_k, "a": transpose_a}[run[0]](*run[1:]))
             pairs = [pair for run in runs for pair in run[0]]
             if slot + 1 < n_items:
-                between = weave(pairs, 4)
-                scores_and_maxima(slot + 1, 0, between)
+                between = weave(pairs, 2)
+                scores_and_maxima(slot + 1, 0, weave([], 1))
                 if slot >= 1:
                     invert_row_sums(slot - 1)
                 scores_and_maxima(slot + 1, 1, between)

from contextlib import ExitStack

import concourse.mybir as mybir
from concourse.masks import make_identity

F32 = mybir.dt.float32
BF16 = mybir.dt.bfloat16
U32 = mybir.dt.uint32
U8 = mybir.dt.uint8
FP8X4 = mybir.dt.float8_e4m3fn_x4
ALU = mybir.AluOpType
FUNC = mybir.ActivationFunctionType
AXIS_X = mybir.AxisListType.X

P = 128
L = 1024
HD = 256
H = 4
KV = 2
D = 1024
PAIR = H // KV
Q_TILES = L // P
K_PASS = 512
BANK = 512
HALF = 256
MASKED = -1.0e30
WO_FIRST = 4
PROJECT_FIRST = 11
V_REGROUP = [0, 3]
WARM_UP = 4
SCALAR_STEP = 16
LAG_V = 3
ORDER = [0, 1, 2, 3, 4, 5, 6, 7]
PROJECT_STEP = 2
AHEAD = 6
LOADS = [(a[0], int(a[1])) for a in "k2 v0 q2 k4 q4 v1 w0 x0 k6 q6 x1 x2 x3 x4 x5 x6 x7".split()]

FLOPS = 2 * H * (512 * 512 + 512 * 1024) * HD * 2 + 2 * L * D * D


def tile_sharedglobalattention_pb_kernel(tc, q_n, k_n, v, Wo, x, gate, log_temperature, out):
    nc = tc.nc
    with ExitStack() as ctx:
        ctx.enter_context(tc.manual_schedule())
        const = ctx.enter_context(tc.tile_pool(name="const", bufs=1))
        resident = ctx.enter_context(tc.tile_pool(name="resident", bufs=1))
        work = ctx.enter_context(tc.tile_pool(name="work", bufs=4))
        small = ctx.enter_context(tc.tile_pool(name="small", bufs=6))
        psum_s = ctx.enter_context(tc.psum_pool(name="psum_s", bufs=4))
        psum_t = ctx.enter_context(tc.psum_pool(name="psum_t", bufs=2))
        psum_acc = ctx.enter_context(tc.psum_pool(name="psum_acc", bufs=2))

        q_raw_first = resident.tile([P, 2, H, HD], BF16, name="q_raw_first")
        q_raw = resident.tile([P, Q_TILES // 2 - 1, KV, PAIR, 2, HD], BF16, name="q_raw")
        k_raw = resident.tile([P, KV, Q_TILES, HD], BF16, name="k_raw")
        v_raw = resident.tile([P, KV * L * HD // P], BF16, name="v_raw")
        wo_raw = resident.tile([P, D * D // P], BF16, name="wo_raw")
        x_sb = resident.tile([P, Q_TILES, D], BF16, name="x_sb")
        q_t_first = resident.tile([P, 2, H, P], F32, name="q_t_first")
        q_t = resident.tile([P, Q_TILES // 2 - 1, KV, PAIR, 2 * P], F32, name="q_t")
        k_t = [resident.tile([P, L], F32, name="k_t%d" % g) for g in range(KV)]
        v_codes = resident.tile([P, KV * 2 * HD], U32, name="v_codes", align_bytes=64)
        v_scales = resident.tile([P, KV * 2 * HD], U8, name="v_scales", align_bytes=64)
        wo_codes = resident.tile([P, 2 * D], U32, name="wo_codes", align_bytes=64)
        wo_scales = resident.tile([P, 2 * D], U8, name="wo_scales", align_bytes=64)
        e_tiles = []
        a_tiles = []
        for i in range(Q_TILES):
            e_tiles.append(resident.tile([P, H, K_PASS * (i // 4 + 1)], BF16, name="e%d" % i))
            a_tiles.append(resident.tile([P, D], BF16, name="a%d" % i))

        scalars = const.tile([P, 2 * SCALAR_STEP], BF16, name="scalars")
        nc.vector.memset(scalars[:], 0.0)

        def load_k(i):
            for g in range(KV):
                nc.sync.dma_start(
                    out=k_raw[:, g, i : i + 2, :],
                    in_=k_n[0, g, i * P : (i + 2) * P, :].rearrange("(p t) d -> p t d", t=2),
                )

        def load_q(i):
            for g in range(KV):
                heads = slice(g * PAIR, (g + 1) * PAIR)
                nc.sync.dma_start(
                    out=q_raw[:, i // 2 - 1, g, :, :, :],
                    in_=q_n[0, heads, i * P : (i + 2) * P, :].rearrange("n (p t) d -> p n t d", t=2),
                )

        def load_q_tile(i, heads):
            nc.sync.dma_start(
                out=q_raw_first[:, i, heads, :], in_=q_n[0, heads, i * P : (i + 1) * P, :].rearrange("n p d -> p n d")
            )

        def load_v(c):
            for g in range(KV):
                cols = slice((g * 2 + c) * 4 * HD, (g * 2 + c + 1) * 4 * HD)
                nc.sync.dma_start(
                    out=v_raw[:, cols].rearrange("p (u e d) -> p u e d", e=2, d=HD),
                    in_=v[0, g, c * K_PASS : (c + 1) * K_PASS, :].rearrange("(u p e) d -> p u e d", p=P, e=2),
                )

        def load_wo(i):
            for g in range(2):
                nc.sync.dma_start(
                    out=wo_raw[:, g * 4 * D : (g + 1) * 4 * D].rearrange("p (u e n) -> p u e n", e=2, n=D),
                    in_=Wo[g * K_PASS : (g + 1) * K_PASS, :].rearrange("(u p e) n -> p u e n", p=P, e=2),
                )

        def load_x(i):
            nc.sync.dma_start(out=x_sb[:, i, :], in_=x[0, i * P : (i + 1) * P, :])

        for g in range(KV):
            nc.sync.dma_start(
                out=k_raw[:, g, 0:2, :], in_=k_n[0, g, 0 : 2 * P, :].rearrange("(t p) d -> p t d", p=P)
            )
            load_q_tile(0, slice(g * PAIR, (g + 1) * PAIR))
        nc.sync.dma_start(out=scalars[0:1, 0:1], in_=log_temperature.unsqueeze(0))
        nc.sync.dma_start(out=scalars[0:1, SCALAR_STEP : SCALAR_STEP + 1], in_=gate.unsqueeze(0))
        load_q_tile(1, slice(0, H))
        for name, arg in LOADS:
            {"q": load_q, "k": load_k, "v": load_v, "x": load_x, "w": load_wo}[name](arg)

        zeros = const.tile([P, BANK], BF16, name="zeros")
        nc.vector.memset(zeros[:].bitcast(F32), 0.0)
        warm = const.tile([P, 1], F32, name="warm")
        nc.vector.memset(warm[:], 0.0)
        nc.scalar.activation(out=warm[:], in_=warm[:], func=FUNC.Exp)
        for i in range(Q_TILES):
            keys = (i + 1) * P
            if keys < K_PASS * (i // 4 + 1):
                words = e_tiles[i][:].rearrange("p h k -> p (h k)").bitcast(F32).rearrange("p (h w) -> p h w", h=H)
                nc.vector.memset(words[:, :, keys // 2 :], 0.0)
        ident_f32 = const.tile([P, P], F32, name="ident_f32")
        make_identity(nc, ident_f32[:])
        ident_bf = const.tile([P, P], BF16, name="ident_bf")
        make_identity(nc, ident_bf[:])
        mask_f32 = const.tile([P, P], F32, name="mask_f32")
        nc.gpsimd.memset(mask_f32[:], 0.0)
        nc.gpsimd.affine_select(
            out=mask_f32[:],
            in_=mask_f32[:],
            compare_op=ALU.is_ge,
            fill=MASKED,
            base=0,
            pattern=[[-1, P]],
            channel_multiplier=1,
        )
        mask_bf = const.tile([P, P], BF16, name="mask_bf")
        nc.vector.tensor_copy(out=mask_bf[:], in_=mask_f32[:])
        ones_bf = const.tile([P, P], BF16, name="ones_bf")
        nc.vector.memset(ones_bf[:], 1.0)
        scale = const.tile([P, 1], F32, name="scale")
        neg_scale = const.tile([P, 1], F32, name="neg_scale")
        gate_f = const.tile([P, 1], F32, name="gate_f")

        def regroup(grouped, raw):
            nc.vector.tensor_copy(
                out=grouped.rearrange("p (c i t) -> p c t i", i=4, t=4), in_=raw.rearrange("p t (c i) -> p c t i", i=4)
            )

        v_grouped = {}

        def regroup_v(g, c):
            cols = slice((g * 2 + c) * 4 * HD, (g * 2 + c + 1) * 4 * HD)
            v_grouped[g] = work.tile([P, 4 * HD], BF16, name="v_grouped", align_bytes=64)
            regroup(v_grouped[g][:], v_raw[:, cols].rearrange("p (t d) -> p t d", t=4))

        def quantise_v(c):
            for g in range(KV):
                cols = slice((g * 2 + c) * HD, (g * 2 + c + 1) * HD)
                nc.vector.quantize_mx(
                    out=v_codes[:, cols].bitcast(FP8X4), scales=v_scales[:, cols], in_=v_grouped[g][:]
                )

        wo_grouped = [resident.tile([P, 4 * BANK], BF16, name="wo_grouped%d" % w, align_bytes=64) for w in range(4)]

        def regroup_wo(w, part, parts, form):
            g, half = w // 2, w % 2
            raw = wo_raw[:, g * 4 * D : (g + 1) * 4 * D].rearrange("p (t n) -> p t n", t=4)
            width = BANK // parts
            form(
                wo_grouped[w][:, part * 4 * width : (part + 1) * 4 * width],
                raw[:, :, half * BANK + part * width : half * BANK + (part + 1) * width],
            )

        def quantise_wo(w):
            cols = slice(w * BANK, (w + 1) * BANK)
            nc.vector.quantize_mx(out=wo_codes[:, cols].bitcast(FP8X4), scales=wo_scales[:, cols], in_=wo_grouped[w][:])

        def halves(words):
            return words.bitcast(BF16).rearrange("p (c e) -> p c e", e=2)

        def transpose_first(g):
            pool, tag = ((psum_t, "t"), (psum_acc, "acc"))[g]
            bank = pool.tile([P, 2, P], F32, name="bank_k0", tag=tag)
            for t in range(2):
                nc.tensor.transpose(bank[:, t, :], k_raw[:, g, t, :].bitcast(F32), ident_f32[:])
            nc.scalar.copy(out=k_t[g][:, : 2 * P].rearrange("p (t k) -> p t k", t=2), in_=bank[:])
            bank = pool.tile([P, PAIR, P], F32, name="bank_q0", tag=tag)
            for h in range(PAIR):
                nc.tensor.transpose(bank[:, h, :], q_raw_first[:, 0, g * PAIR + h, :].bitcast(F32), ident_f32[:])
            nc.vector.tensor_copy(out=q_t_first[:, 0, g * PAIR : (g + 1) * PAIR, :], in_=bank[:])

        def transpose_second():
            bank = psum_t.tile([P, H, P], F32, name="bank_q1", tag="t")
            for n in range(H):
                nc.tensor.transpose(bank[:, n, :], q_raw_first[:, 1, n, :].bitcast(F32), ident_f32[:])
            nc.scalar.copy(out=q_t_first[:, 1, :, :], in_=bank[:])

        def transpose_q(i, g):
            bank = psum_t.tile([P, PAIR, 2, P], F32, name="bank_q", tag="t")
            pairs = []
            for h in range(PAIR):
                for t in range(2):
                    pairs.append((bank[:, h, t, :], q_raw[:, i // 2 - 1, g, h, t, :].bitcast(F32)))
            return pairs, lambda: nc.scalar.copy(
                out=q_t[:, i // 2 - 1, g, :, :].rearrange("p h (k t) -> p h k t", t=2),
                in_=bank[:].rearrange("p h t k -> p h k t"),
            )

        def transpose_k(i):
            bank = psum_t.tile([P, KV, 2, P], F32, name="bank_k", tag="t")
            pairs = []
            for g in range(KV):
                for t in range(2):
                    pairs.append((bank[:, g, t, :], k_raw[:, g, i + t, :].bitcast(F32)))

            def copy():
                for g in range(KV):
                    nc.scalar.copy(
                        out=k_t[g][:, i * P : (i + 2) * P].rearrange("p (k t) -> p k t", t=2),
                        in_=bank[:, g, :, :].rearrange("p t k -> p k t"),
                    )

            return pairs, copy

        items = []
        first_item = [0] * Q_TILES
        last_item = [0] * Q_TILES
        for i in ORDER:
            first_item[i] = len(items)
            for g in range(KV):
                if i < 4:
                    items.append((i, g, [0, 1], [0]))
                else:
                    items.append((i, g, [0], [0, 1]))
                    items.append((i, g, [1], [0, 1]))
            last_item[i] = len(items) - 1
        n_items = len(items)
        live = {}

        def scores_and_maxima(j, piece, between):
            i, g, heads, chunks = items[j]
            keys = (i + 1) * P
            h, c = [(h, c) for h in heads for c in chunks][piece]
            if piece == 0:
                live[j] = {"banks": [], "maxima": small.tile([P, 2], F32, name="maxima")}
            maxima = live[j]["maxima"]
            width = min(K_PASS, keys - c * K_PASS)
            s = psum_s.tile([P, BANK], F32, name="s")
            diagonal = c == chunks[-1]
            if i < 2:
                queries = q_t_first[:, i, g * PAIR + h, :]
            else:
                queries = q_t[:, i // 2 - 1, g, h, i % 2 * P : (i % 2 + 1) * P]
            for e in range(2):
                nc.tensor.matmul(
                    s[:, :width],
                    lhsT=halves(queries)[:, :, e],
                    rhs=halves(k_t[g][:, c * K_PASS : c * K_PASS + width])[:, :, e],
                    start=(e == 0),
                    stop=(e == 1 and not diagonal),
                )
                between()
            if diagonal:
                nc.tensor.matmul(s[:, width - P : width], lhsT=ident_bf[:], rhs=mask_bf[:], start=False, stop=True)
            nc.vector.tensor_reduce(out=maxima[:, piece : piece + 1], in_=s[:, :width], axis=AXIS_X, op=ALU.max)
            live[j]["banks"].append((s, width))

        def biases(j):
            i, g, heads, chunks = items[j]
            maxima = live[j]["maxima"]
            bias = small.tile([P, 2], F32, name="bias")
            if len(chunks) == 2:
                nc.vector.tensor_scalar(
                    out=bias[:, 0:1], in0=maxima[:, 0:1], scalar1=maxima[:, 1:2], scalar2=neg_scale[:, 0:1],
                    op0=ALU.max, op1=ALU.mult,
                )
            else:
                nc.vector.tensor_scalar(
                    out=bias[:], in0=maxima[:], scalar1=neg_scale[:, 0:1], scalar2=None, op0=ALU.mult
                )
            live[j]["bias"] = bias

        def exponentials(j):
            i, g, heads, chunks = items[j]
            if len(chunks) == 1 or heads[0] == 0:
                row_sums = small.tile([P, PAIR, len(chunks)], F32, name="row_sums")
            else:
                row_sums = live[j - 1]["row_sums"]
            piece = 0
            for h in heads:
                for c in chunks:
                    s, width = live[j]["banks"][piece]
                    nc.scalar.activation(
                        out=e_tiles[i][:, g * PAIR + h, c * K_PASS : c * K_PASS + width],
                        in_=s[:, :width],
                        func=FUNC.Exp,
                        bias=live[j]["bias"][:, heads.index(h) : heads.index(h) + 1],
                        scale=scale[:, 0:1],
                        accum_out=row_sums[:, h, c : c + 1],
                    )
                    piece += 1
            live[j]["row_sums"] = row_sums

        def transpose_bank(n, draining):
            if draining:
                return psum_s.tile([P, n, 2, P], F32, name="bank_drain", tag="s")
            return psum_t.tile([P, n, 2, P], F32, name="bank", tag="t")

        def copy_out(grouped, bank, n, on_vector):
            out, in_ = grouped.rearrange("p (s q u) -> p s q u", s=n, u=2), bank[:].rearrange("p s u q -> p s q u")
            if on_vector:
                nc.vector.tensor_copy(out=out, in_=in_)
            else:
                nc.scalar.copy(out=out, in_=in_)

        def transpose_e(j, pieces=(0, 1), draining=False):
            i, g, heads, chunks = items[j]
            n_pieces = len(pieces)
            bank = transpose_bank(n_pieces, draining)
            pairs = []
            for piece in pieces:
                h, c = [(h, c) for h in heads for c in chunks][piece]
                for u in range(2):
                    first_key = c * K_PASS + u * HALF
                    keys = e_tiles[i][:, g * PAIR + h, first_key : first_key + HALF]
                    pairs.append((bank[:, piece - pieces[0], u, :], keys.bitcast(F32)))
            if pieces[0] == 0:
                live[j]["e_grouped"] = work.tile([P, 2 * P * 2], F32, name="e_grouped", align_bytes=64)
            words = live[j]["e_grouped"][:, pieces[0] * P * 2 : (pieces[-1] + 1) * P * 2]
            return pairs, lambda: copy_out(words, bank, n_pieces, j == n_items - 2)

        def quantise_e(j, pieces=(0, 1)):
            if pieces[0] == 0:
                live[j]["e_codes"] = work.tile([P, 2 * P], U32, name="e_codes", align_bytes=64)
                live[j]["e_scales"] = work.tile([P, 2 * P], U8, name="e_scales", align_bytes=64)
            cols = slice(pieces[0] * P, (pieces[-1] + 1) * P)
            words = live[j]["e_grouped"][:, pieces[0] * P * 2 : (pieces[-1] + 1) * P * 2]
            nc.vector.quantize_mx(
                out=live[j]["e_codes"][:, cols].bitcast(FP8X4),
                scales=live[j]["e_scales"][:, cols],
                in_=words.bitcast(BF16),
            )

        def add_row_sums(j):
            i, g, heads, chunks = items[j]
            row_sums = live[j]["row_sums"]
            if len(chunks) == 1:
                live[j]["total"] = row_sums[:, :, 0]
            elif heads[0] == 1:
                total = small.tile([P, PAIR], F32, name="total")
                nc.vector.tensor_tensor(out=total[:], in0=row_sums[:, :, 0], in1=row_sums[:, :, 1], op=ALU.add)
                live[j]["total"] = total[:]

        def invert_row_sums(j):
            if "total" in live[j]:
                inverse = small.tile([P, PAIR], F32, name="inverse")
                nc.vector.reciprocal(out=inverse[:], in_=live[j]["total"])
                for pair_item in (j,) if len(items[j][3]) == 1 else (j - 1, j):
                    live[pair_item]["inverse"] = inverse

        def accumulator(shape, draining):
            if draining:
                return psum_s.tile(shape, F32, name="acc_drain", tag="s")
            return psum_acc.tile(shape, F32, name="acc", tag="acc")

        def multiply_v(j, draining=False):
            i, g, heads, chunks = items[j]
            o = accumulator([P, 2, HD], draining)
            piece = 0
            for h in heads:
                for c in chunks:
                    v_cols = slice((g * 2 + c) * HD, (g * 2 + c + 1) * HD)
                    nc.tensor.matmul_mx(
                        out=o[:, heads.index(h), :],
                        lhsT=live[j]["e_codes"][:, piece * P : (piece + 1) * P].bitcast(FP8X4),
                        lhsT_scale=live[j]["e_scales"][:, piece * P : (piece + 1) * P],
                        rhs=v_codes[:, v_cols].bitcast(FP8X4),
                        rhs_scale=v_scales[:, v_cols],
                        start=(c == chunks[0]),
                        stop=(c == chunks[-1]),
                    )
                    piece += 1
            live[j]["o"] = o

        def normalise(j):
            i, g, heads, chunks = items[j]
            o, inverse = live[j]["o"], live[j]["inverse"]
            for h in heads:
                n = g * PAIR + h
                nc.scalar.activation(
                    out=a_tiles[i][:, n * HD : (n + 1) * HD],
                    in_=o[:, heads.index(h), :],
                    func=FUNC.Copy,
                    scale=inverse[:, h : h + 1],
                )

        projecting = {}

        def transpose_a(i, passes=(0, 1), draining=False):
            n_passes = len(passes)
            bank = transpose_bank(n_passes, draining)
            pairs = []
            for g in passes:
                for u in range(2):
                    first = g * K_PASS + u * HALF
                    pairs.append((bank[:, g - passes[0], u, :], a_tiles[i][:, first : first + HALF].bitcast(F32)))
            if passes[0] == 0:
                projecting[i] = {"a_grouped": work.tile([P, 2 * P * 2], F32, name="a_grouped", align_bytes=64)}
            words = projecting[i]["a_grouped"][:, passes[0] * P * 2 : (passes[-1] + 1) * P * 2]
            return pairs, lambda: copy_out(words, bank, n_passes, i == ORDER[-2])

        def quantise_a(i, passes=(0, 1)):
            if passes[0] == 0:
                projecting[i]["a_codes"] = work.tile([P, 2 * P], U32, name="a_codes", align_bytes=64)
                projecting[i]["a_scales"] = work.tile([P, 2 * P], U8, name="a_scales", align_bytes=64)
                projecting[i]["result"] = work.tile([P, D], F32, name="result")
            cols = slice(passes[0] * P, (passes[-1] + 1) * P)
            words = projecting[i]["a_grouped"][:, passes[0] * P * 2 : (passes[-1] + 1) * P * 2]
            nc.vector.quantize_mx(
                out=projecting[i]["a_codes"][:, cols].bitcast(FP8X4),
                scales=projecting[i]["a_scales"][:, cols],
                in_=words.bitcast(BF16),
            )

        def project(i, half, passes=(0, 1), draining=False):
            if passes[0] == 0:
                projecting[i][half] = accumulator([P, BANK], draining)
            acc = projecting[i][half]
            for g in passes:
                w_cols = slice(g * D + half * BANK, g * D + (half + 1) * BANK)
                nc.tensor.matmul_mx(
                    out=acc[:],
                    lhsT=projecting[i]["a_codes"][:, g * P : (g + 1) * P].bitcast(FP8X4),
                    lhsT_scale=projecting[i]["a_scales"][:, g * P : (g + 1) * P],
                    rhs=wo_codes[:, w_cols].bitcast(FP8X4),
                    rhs_scale=wo_scales[:, w_cols],
                    start=(g == 0),
                    stop=(g == 1),
                )

        def add_residual(i, half, parts=1):
            result = projecting[i]["result"]
            width = BANK // parts
            for part in range(parts):
                bank_cols = slice(part * width, (part + 1) * width)
                cols = slice(half * BANK + part * width, half * BANK + (part + 1) * width)
                nc.vector.scalar_tensor_tensor(
                    out=result[:, cols], in0=projecting[i][half][:, bank_cols], scalar=gate_f[:, 0:1],
                    in1=x_sb[:, i, cols], op0=ALU.mult, op1=ALU.add,
                )
                nc.sync.dma_start(out=out[0, i * P : (i + 1) * P, cols], in_=result[:, cols])

        other_run = {}
        needs = []
        for i in range(2, Q_TILES, 2):
            needs.append((first_item[i], ("k", i)))
            for g in range(KV):
                needs.append((first_item[i] + g * (1 if i < 4 else 2), ("q", i, g)))
        for need, run in sorted(needs):
            slot = max(need - AHEAD, 0)
            while slot > 0 and (slot in other_run or (slot >= PROJECT_FIRST and slot % 2 == PROJECT_FIRST % 2)):
                slot = slot - 1
            while slot in other_run:
                slot = slot + 1
            other_run[slot] = run
        project_slot = {}
        earliest = PROJECT_FIRST
        for i in ORDER[:-2]:
            slot = max(last_item[i] + LAG_V + 1, earliest)
            while slot in other_run:
                slot = slot + 1
            other_run[slot] = ("a", i)
            project_slot[slot] = i
            earliest = slot + PROJECT_STEP
        dummy = psum_s.tile([P, BANK], F32, name="dummy", tag="s")
        for n in range(WARM_UP):
            nc.tensor.matmul(dummy[:], lhsT=zeros[:, :P], rhs=zeros[:], start=True, stop=True)
        transpose_first(0)
        transpose_first(1)
        spread = psum_s.tile([P, 2 * SCALAR_STEP], F32, name="spread", tag="s")
        nc.tensor.matmul(spread[:], lhsT=ones_bf[:], rhs=scalars[:], start=True, stop=True)
        nc.scalar.activation(out=scale[:], in_=spread[:, 0:1], func=FUNC.Exp)
        nc.vector.tensor_copy(out=gate_f[:], in_=spread[:, SCALAR_STEP : SCALAR_STEP + 1])
        nc.vector.tensor_scalar(out=neg_scale[:], in0=scale[:], scalar1=-1.0, scalar2=None, op0=ALU.mult)
        def weave(pairs, gaps):
            calls = []

            def between():
                n = len(calls)
                calls.append(n)
                if n < gaps:
                    for out_words, in_words in pairs[len(pairs) * n // gaps : len(pairs) * (n + 1) // gaps]:
                        nc.tensor.transpose(out_words, in_words, ident_f32[:])

            return between

        def transpose_now(run):
            pairs, copy = run
            weave(pairs, 1)()
            copy()

        scores_and_maxima(0, 0, weave([], 1))
        scores_and_maxima(0, 1, weave([], 1))
        biases(0)
        transpose_second()
        for slot in range(0, n_items):
            if 0 <= slot - 1 < n_items:
                add_row_sums(slot - 1)
            if slot - 1 in project_slot:
                quantise_a(project_slot[slot - 1])
            exponentials(slot)
            runs = []
            if slot >= 1:
                runs.append(transpose_e(slot - 1))
            if slot in other_run:
                run = other_run[slot]
                runs.append({"q": transpose_q, "k": transpose_k, "a": transpose_a}[run[0]](*run[1:]))
            pairs = [pair for run in runs for pair in run[0]]
            if slot + 1 < n_items:
                between = weave(pairs, 2)
                scores_and_maxima(slot + 1, 0, weave([], 1))
                if slot >= 1:
                    invert_row_sums(slot - 1)
                scores_and_maxima(slot + 1, 1, between)
            else:
                invert_row_sums(slot - 1)
                weave(pairs, 1)()
            for run in runs:
                run[1]()
            if 0 <= slot - 2 < n_items:
                quantise_e(slot - 2)
            if slot + 1 < n_items:
                biases(slot + 1)
            if slot >= LAG_V:
                multiply_v(slot - LAG_V)
                normalise(slot - LAG_V)
            for g in range(KV):
                for c in range(2):
                    if slot == V_REGROUP[c] + g:
                        regroup_v(g, c)
            for c in range(2):
                if slot == V_REGROUP[c] + 2:
                    quantise_v(c)
            quarters = [0, 2, 1, 3]
            if 0 <= slot - WO_FIRST < 8:
                regroup_wo(quarters[(slot - WO_FIRST) // 2], (slot - WO_FIRST) % 2, 2, regroup)
            if 0 <= slot - WO_FIRST - 2 < 8 and (slot - WO_FIRST) % 2 == 0:
                quantise_wo(quarters[(slot - WO_FIRST - 2) // 2])
            for half in range(2):
                if slot - 1 - half in project_slot:
                    project(project_slot[slot - 1 - half], half, draining=(slot == n_items - 1))
                    add_residual(project_slot[slot - 1 - half], half)

        last = n_items - 1
        before, final = ORDER[-2], ORDER[-1]
        transpose_now(transpose_e(last, (0,), True))
        transpose_now(transpose_e(last, (1,), True))
        quantise_e(last - 1)
        multiply_v(last - 2)
        normalise(last - 2)
        add_row_sums(last)
        quantise_e(last, (0,))
        quantise_e(last, (1,))
        invert_row_sums(last)
        transpose_now(transpose_a(before))
        multiply_v(last - 1)
        normalise(last - 1)
        multiply_v(last, True)
        normalise(last)
        quantise_a(before)
        transpose_now(transpose_a(final, (0,)))
        quantise_a(final, (0,))
        transpose_now(transpose_a(final, (1,), True))
        quantise_a(final, (1,))
        for half in range(2):
            project(before, half)
            add_residual(before, half)
        for half in range(2):
            project(final, half, (0,), True)
        for half in range(2):
            project(final, half, (1,), True)
            add_residual(final, half, 1 + half)
